import numpy as np
import ml_dtypes


def mxq(x, axis, fmt="e4m3"):
    dtype, down = {"e4m3": (ml_dtypes.float8_e4m3fn, 7), "e5m2": (ml_dtypes.float8_e5m2, 14)}[fmt]
    v = np.moveaxis(np.asarray(x, np.float32).astype(ml_dtypes.bfloat16).astype(np.float64), axis, -1)
    blocks = v.reshape(v.shape[:-1] + (-1, 32))
    amax = np.abs(blocks).max(-1, keepdims=True)
    byte = np.maximum(np.where(amax > 0, np.frexp(amax)[1] - 1 + 127, 0) - down, 1)
    scale = np.exp2(byte - 127.0)
    codes = (blocks / scale).astype(np.float32).astype(dtype).astype(np.float64)
    return np.moveaxis((codes * scale).reshape(v.shape), -1, axis)


WIDE = False


def mx_kscale(k):
    if not WIDE:
        return np.ones(k)
    levels = np.array([10, -10, 5, -5, 0])
    a = np.random.permutation(np.resize(levels, k // 512 * 4)).reshape(k // 512, 4)
    idx = np.arange(k)
    return np.exp2(a[idx // 512, idx % 128 // 32])


BF16 = ml_dtypes.bfloat16


def bf(x):
    return np.asarray(x, np.float32).astype(BF16)


def f64(x):
    return np.asarray(x).astype(np.float64)


B, SEQ, C, P, H, W = 2, 8, 1024, 512, 8, 8
L = SEQ * H * W
A = np.sqrt(2.0) / P ** 0.25


def setup_inputs():
    s, u = mx_kscale(C), mx_kscale(P)
    return {"x": bf(np.random.standard_normal((B * SEQ, C, H, W)) * s[None, :, None, None]),
            "t_w": bf(np.random.standard_normal((P, C)) * A / np.sqrt(C) / s[None, :] * u[:, None]),
            "t_b": bf(np.random.standard_normal(P) * 0.1 * u),
            "p_w": bf(np.random.standard_normal((P, C)) * A / np.sqrt(C) / s[None, :] / u[:, None]),
            "p_b": bf(np.random.standard_normal(P) * 0.1 / u)}


def reference(x, t_w, t_b, p_w, p_b):
    xl = f64(x).reshape(B, SEQ, C, H * W).transpose(0, 1, 3, 2).reshape(B, L, C)
    xq = mxq(xl, 2, "e4m3")
    t = (xq @ mxq(f64(t_w), 1, "e4m3").T) + f64(t_b)
    p = (xq @ mxq(f64(p_w), 1, "e4m3").T) + f64(p_b)
    return mxq(t, 2, "e4m3") @ mxq(p, 2, "e4m3").transpose(0, 2, 1)

@@ -1,0 +1,178 @@
+from contextlib import ExitStack
+
+import concourse.mybir as mybir
+from concourse.masks import make_identity
+
+BF16 = mybir.dt.bfloat16
+F32 = mybir.dt.float32
+U32 = mybir.dt.uint32
+U8 = mybir.dt.uint8
+FP8X4 = mybir.dt.float8_e4m3fn_x4
+ADD = mybir.AluOpType.add
+
+P = 128
+PACK = 4
+K_PASS = P * PACK
+
+CLIPS = 2
+FRAMES = 8
+GRID = 64
+L = FRAMES * GRID
+C = 1024
+C_PASSES = C // K_PASS
+FEATURES = 512
+FEATURE_TILES = FEATURES // P
+
+QUAD_FRAMES = 4
+QUAD = QUAD_FRAMES * GRID
+QUADS = CLIPS * L // QUAD
+QUADS_PER_CLIP = L // QUAD
+CHUNK = 128
+CHUNKS_PER_QUAD = QUAD // CHUNK
+ROW_TILES = L // P
+
+FLOPS = 2 * 2 * CLIPS * L * C * FEATURES + 2 * CLIPS * L * L * FEATURES
+
+
+def tile_stnonlocalgnlstage_pa_kernel(tc, x, t_w, t_b, p_w, p_b, out):
+    nc = tc.nc
+    with ExitStack() as stack:
+        keep = stack.enter_context(tc.tile_pool(name="keep", bufs=1))
+        psum_w = stack.enter_context(tc.psum_pool(name="psum_w", bufs=2))
+        psum_tp = stack.enter_context(tc.psum_pool(name="psum_tp", bufs=4))
+        psum_out = stack.enter_context(tc.psum_pool(name="psum_out", bufs=2))
+
+        identity = keep.tile([P, P], F32, name="identity")
+        make_identity(nc, identity[:])
+
+        w_raw = {}
+        bias = {}
+        for which, w, b in (("t", t_w, t_b), ("p", p_w, p_b)):
+            w_raw[which] = keep.tile([P, FEATURE_TILES * C], BF16, name="w_raw_%s" % which)
+            w_rows = w.rearrange("(p m) c -> p (m c)", m=FEATURE_TILES)
+            half = FEATURE_TILES * C // 2
+            for cols in (slice(0, half), slice(half, 2 * half)):
+                nc.sync.dma_start(out=w_raw[which][:, cols], in_=w_rows[:, cols])
+            bias[which] = keep.tile([P, FEATURE_TILES], BF16, name="bias_%s" % which)
+            nc.scalar.dma_start(out=bias[which][:], in_=b.rearrange("(p m) -> p m", m=FEATURE_TILES))
+
+        x_raw = []
+        for q in range(QUADS):
+            raw = keep.tile([P, C_PASSES, QUAD_FRAMES, PACK * GRID], BF16, name="x_raw_%d" % q)
+            frames = slice(q * QUAD_FRAMES, (q + 1) * QUAD_FRAMES)
+            for g in range(C_PASSES):
+                channels = slice(g * K_PASS, (g + 1) * K_PASS)
+                nc.sync.dma_start(
+                    out=raw[:, g],
+                    in_=x[frames, channels].rearrange("f (p j) h w -> p f (j h w)", j=PACK),
+                )
+            x_raw.append(raw)
+
+        w_codes = {}
+        w_scales = {}
+        for which in ("t", "p"):
+            words = w_raw[which][:].bitcast(F32).rearrange(
+                "p (m g n u) -> p m g u n", m=FEATURE_TILES, g=C_PASSES, u=2
+            )
+            w_codes[which] = keep.tile(
+                [P, FEATURE_TILES, C_PASSES, P], U32, align_bytes=64, name="w_codes_%s" % which
+            )
+            w_scales[which] = keep.tile(
+                [P, FEATURE_TILES, C_PASSES, P], U8, align_bytes=64, name="w_scales_%s" % which
+            )
+            for m in range(FEATURE_TILES):
+                flipped = psum_w.tile([P, C_PASSES, 2, P], F32, name="flipped")
+                for g in range(C_PASSES):
+                    for u in range(2):
+                        nc.tensor.transpose(
+                            out=flipped[:, g, u, :],
+                            in_=words[:, m, g, u, :],
+                            identity=identity[:],
+                        )
+                w_grouped = keep.tile(
+                    [P, C_PASSES * P * PACK], BF16, align_bytes=64, name="w_grouped_%s%d" % (which, m)
+                )
+                copy = nc.scalar.copy if m % 2 == 0 else nc.vector.tensor_copy
+                copy(
+                    out=w_grouped[:].bitcast(F32).rearrange("p (g n u) -> p g n u", g=C_PASSES, u=2),
+                    in_=flipped[:].rearrange("p g u n -> p g n u"),
+                )
+                nc.vector.quantize_mx(
+                    out=w_codes[which][:, m].rearrange("p g n -> p (g n)").bitcast(FP8X4),
+                    scales=w_scales[which][:, m].rearrange("p g n -> p (g n)"),
+                    in_=w_grouped[:],
+                )
+
+        tp_grouped = {}
+        tp_codes = {}
+        tp_scales = {}
+        for q in range(QUADS):
+            clip = q // QUADS_PER_CLIP
+            x_grouped = keep.tile([P, C_PASSES, QUAD, PACK], BF16, align_bytes=64, name="x_grouped_%d" % q)
+            x_codes = keep.tile([P, C_PASSES, QUAD], U32, align_bytes=64, name="x_codes_%d" % q)
+            x_scales = keep.tile([P, C_PASSES, QUAD], U8, align_bytes=64, name="x_scales_%d" % q)
+            for g in range(C_PASSES):
+                nc.scalar.copy(
+                    out=x_grouped[:, g].rearrange("p (f s) j -> p f s j", f=QUAD_FRAMES),
+                    in_=x_raw[q][:, g].rearrange("p f (j s) -> p f s j", j=PACK),
+                )
+                nc.vector.quantize_mx(
+                    out=x_codes[:, g].bitcast(FP8X4),
+                    scales=x_scales[:, g],
+                    in_=x_grouped[:, g].rearrange("p s j -> p (s j)"),
+                )
+
+            if q % QUADS_PER_CLIP == 0:
+                for which in ("t", "p"):
+                    tp_grouped[which] = keep.tile(
+                        [P, L, PACK], BF16, align_bytes=64, name="grouped_%s%d" % (which, clip)
+                    )
+                    tp_codes[which] = keep.tile([P, L], U32, align_bytes=64, name="codes_%s%d" % (which, clip))
+                    tp_scales[which] = keep.tile([P, L], U8, align_bytes=64, name="scales_%s%d" % (which, clip))
+
+            for h in range(CHUNKS_PER_QUAD):
+                in_quad = slice(h * CHUNK, (h + 1) * CHUNK)
+                first = (q % QUADS_PER_CLIP) * QUAD + h * CHUNK
+                in_clip = slice(first, first + CHUNK)
+                for which in ("t", "p"):
+                    acc = psum_tp.tile([P, FEATURE_TILES, CHUNK], F32, name="acc")
+                    for m in range(FEATURE_TILES):
+                        for g in range(C_PASSES):
+                            nc.tensor.matmul_mx(
+                                out=acc[:, m, :],
+                                lhsT=w_codes[which][:, m, g, :].bitcast(FP8X4),
+                                lhsT_scale=w_scales[which][:, m, g, :],
+                                rhs=x_codes[:, g, in_quad].bitcast(FP8X4),
+                                rhs_scale=x_scales[:, g, in_quad],
+                                start=(g == 0),
+                                stop=(g == C_PASSES - 1),
+                            )
+                    nc.vector.tensor_tensor(
+                        out=tp_grouped[which][:, in_clip, :],
+                        in0=acc[:].rearrange("p m r -> p r m"),
+                        in1=bias[which][:].unsqueeze(1).to_broadcast([P, CHUNK, FEATURE_TILES]),
+                        op=ADD,
+                    )
+                for which in ("t", "p"):
+                    nc.vector.quantize_mx(
+                        out=tp_codes[which][:, in_clip].bitcast(FP8X4),
+                        scales=tp_scales[which][:, in_clip],
+                        in_=tp_grouped[which][:, in_clip, :].rearrange("p r m -> p (r m)"),
+                    )
+
+            if q % QUADS_PER_CLIP == QUADS_PER_CLIP - 1:
+                for i in range(ROW_TILES):
+                    rows = slice(i * P, (i + 1) * P)
+                    affinity = psum_out.tile([P, L], F32, name="affinity")
+                    nc.tensor.matmul_mx(
+                        out=affinity[:],
+                        lhsT=tp_codes["t"][:, rows].bitcast(FP8X4),
+                        lhsT_scale=tp_scales["t"][:, rows],
+                        rhs=tp_codes["p"][:].bitcast(FP8X4),
+                        rhs_scale=tp_scales["p"][:],
+                        start=True,
+                        stop=True,
+                    )
+                    result = keep.tile([P, L], F32, name="result_%d_%d" % (clip, i))
+                    nc.scalar.copy(out=result[:], in_=affinity[:])
+                    nc.sync.dma_start(out=out[clip, rows, :], in_=result[:])

@@ -15,9 +15,8 @@ PACK = 4
 K_PASS = P * PACK
 
 CLIPS = 2
-FRAMES = 8
 GRID = 64
-L = FRAMES * GRID
+L = 512
 C = 1024
 C_PASSES = C // K_PASS
 FEATURES = 512
@@ -25,11 +24,10 @@ FEATURE_TILES = FEATURES // P
 
 QUAD_FRAMES = 4
 QUAD = QUAD_FRAMES * GRID
-QUADS = CLIPS * L // QUAD
 QUADS_PER_CLIP = L // QUAD
 CHUNK = 128
+CHUNKS = L // CHUNK
 CHUNKS_PER_QUAD = QUAD // CHUNK
-ROW_TILES = L // P
 
 FLOPS = 2 * 2 * CLIPS * L * C * FEATURES + 2 * CLIPS * L * L * FEATURES
 
@@ -38,41 +36,38 @@ def tile_stnonlocalgnlstage_pa_kernel(tc, x, t_w, t_b, p_w, p_b, out):
     nc = tc.nc
     with ExitStack() as stack:
         keep = stack.enter_context(tc.tile_pool(name="keep", bufs=1))
-        psum_w = stack.enter_context(tc.psum_pool(name="psum_w", bufs=2))
+        psum_wide = stack.enter_context(tc.psum_pool(name="psum_wide", bufs=4))
         psum_tp = stack.enter_context(tc.psum_pool(name="psum_tp", bufs=4))
-        psum_out = stack.enter_context(tc.psum_pool(name="psum_out", bufs=2))
 
         identity = keep.tile([P, P], F32, name="identity")
         make_identity(nc, identity[:])
 
-        w_raw = {}
-        bias = {}
-        for which, w, b in (("t", t_w, t_b), ("p", p_w, p_b)):
+        w_raw, bias, w_codes, w_scales = {}, {}, {}, {}
+        x_raw, x_codes, x_scales = {}, {}, {}
+        acc, tp_grouped, tp_codes, tp_scales = {}, {}, {}, {}
+
+        def load_weight(which, w, b):
             w_raw[which] = keep.tile([P, FEATURE_TILES * C], BF16, name="w_raw_%s" % which)
-            w_rows = w.rearrange("(p m) c -> p (m c)", m=FEATURE_TILES)
-            half = FEATURE_TILES * C // 2
-            for cols in (slice(0, half), slice(half, 2 * half)):
+            w_rows = w.rearrange("(n m) c -> n (m c)", m=FEATURE_TILES)
+            for m in range(FEATURE_TILES):
+                cols = slice(m * C, (m + 1) * C)
                 nc.sync.dma_start(out=w_raw[which][:, cols], in_=w_rows[:, cols])
             bias[which] = keep.tile([P, FEATURE_TILES], BF16, name="bias_%s" % which)
-            nc.scalar.dma_start(out=bias[which][:], in_=b.rearrange("(p m) -> p m", m=FEATURE_TILES))
+            nc.scalar.dma_start(out=bias[which][:], in_=b.rearrange("(n m) -> n m", m=FEATURE_TILES))
 
-        x_raw = []
-        for q in range(QUADS):
-            raw = keep.tile([P, C_PASSES, QUAD_FRAMES, PACK * GRID], BF16, name="x_raw_%d" % q)
-            frames = slice(q * QUAD_FRAMES, (q + 1) * QUAD_FRAMES)
+        def load_x(quad):
+            x_raw[quad] = keep.tile([P, C_PASSES, QUAD_FRAMES, PACK * GRID], BF16, name="x_raw_%d" % quad)
+            frames = slice(quad * QUAD_FRAMES, (quad + 1) * QUAD_FRAMES)
             for g in range(C_PASSES):
                 channels = slice(g * K_PASS, (g + 1) * K_PASS)
                 nc.sync.dma_start(
-                    out=raw[:, g],
-                    in_=x[frames, channels].rearrange("f (p j) h w -> p f (j h w)", j=PACK),
+                    out=x_raw[quad][:, g],
+                    in_=x[frames, channels].rearrange("f (q j) h w -> q f (j h w)", j=PACK),
                 )
-            x_raw.append(raw)
 
-        w_codes = {}
-        w_scales = {}
-        for which in ("t", "p"):
+        def prepare_weight(which):
             words = w_raw[which][:].bitcast(F32).rearrange(
-                "p (m g n u) -> p m g u n", m=FEATURE_TILES, g=C_PASSES, u=2
+                "n (m g q u) -> n m g u q", m=FEATURE_TILES, g=C_PASSES, u=2
             )
             w_codes[which] = keep.tile(
                 [P, FEATURE_TILES, C_PASSES, P], U32, align_bytes=64, name="w_codes_%s" % which
@@ -81,98 +76,119 @@ def tile_stnonlocalgnlstage_pa_kernel(tc, x, t_w, t_b, p_w, p_b, out):
                 [P, FEATURE_TILES, C_PASSES, P], U8, align_bytes=64, name="w_scales_%s" % which
             )
             for m in range(FEATURE_TILES):
-                flipped = psum_w.tile([P, C_PASSES, 2, P], F32, name="flipped")
+                flipped = psum_wide.tile([P, C_PASSES, 2, P], F32, name="flipped", tag="wide")
                 for g in range(C_PASSES):
                     for u in range(2):
                         nc.tensor.transpose(
-                            out=flipped[:, g, u, :],
-                            in_=words[:, m, g, u, :],
-                            identity=identity[:],
+                            out=flipped[:, g, u, :], in_=words[:, m, g, u, :], identity=identity[:]
                         )
                 w_grouped = keep.tile(
                     [P, C_PASSES * P * PACK], BF16, align_bytes=64, name="w_grouped_%s%d" % (which, m)
                 )
-                copy = nc.scalar.copy if m % 2 == 0 else nc.vector.tensor_copy
-                copy(
-                    out=w_grouped[:].bitcast(F32).rearrange("p (g n u) -> p g n u", g=C_PASSES, u=2),
-                    in_=flipped[:].rearrange("p g u n -> p g n u"),
+                nc.scalar.copy(
+                    out=w_grouped[:].bitcast(F32).rearrange("q (g n u) -> q g n u", g=C_PASSES, u=2),
+                    in_=flipped[:].rearrange("q g u n -> q g n u"),
                 )
                 nc.vector.quantize_mx(
-                    out=w_codes[which][:, m].rearrange("p g n -> p (g n)").bitcast(FP8X4),
-                    scales=w_scales[which][:, m].rearrange("p g n -> p (g n)"),
+                    out=w_codes[which][:, m].rearrange("q g n -> q (g n)").bitcast(FP8X4),
+                    scales=w_scales[which][:, m].rearrange("q g n -> q (g n)"),
                     in_=w_grouped[:],
                 )
 
-        tp_grouped = {}
-        tp_codes = {}
-        tp_scales = {}
-        for q in range(QUADS):
-            clip = q // QUADS_PER_CLIP
-            x_grouped = keep.tile([P, C_PASSES, QUAD, PACK], BF16, align_bytes=64, name="x_grouped_%d" % q)
-            x_codes = keep.tile([P, C_PASSES, QUAD], U32, align_bytes=64, name="x_codes_%d" % q)
-            x_scales = keep.tile([P, C_PASSES, QUAD], U8, align_bytes=64, name="x_scales_%d" % q)
+        def prepare_x(quad, copy):
+            x_grouped = keep.tile([P, C_PASSES, QUAD, PACK], BF16, align_bytes=64, name="x_grouped_%d" % quad)
+            x_codes[quad] = keep.tile([P, C_PASSES, QUAD], U32, align_bytes=64, name="x_codes_%d" % quad)
+            x_scales[quad] = keep.tile([P, C_PASSES, QUAD], U8, align_bytes=64, name="x_scales_%d" % quad)
             for g in range(C_PASSES):
-                nc.scalar.copy(
-                    out=x_grouped[:, g].rearrange("p (f s) j -> p f s j", f=QUAD_FRAMES),
-                    in_=x_raw[q][:, g].rearrange("p f (j s) -> p f s j", j=PACK),
+                copy(
+                    out=x_grouped[:, g].rearrange("q (f s) j -> q f s j", f=QUAD_FRAMES),
+                    in_=x_raw[quad][:, g].rearrange("q f (j s) -> q f s j", j=PACK),
                 )
+            for g in range(C_PASSES):
                 nc.vector.quantize_mx(
-                    out=x_codes[:, g].bitcast(FP8X4),
-                    scales=x_scales[:, g],
-                    in_=x_grouped[:, g].rearrange("p s j -> p (s j)"),
+                    out=x_codes[quad][:, g].bitcast(FP8X4),
+                    scales=x_scales[quad][:, g],
+                    in_=x_grouped[:, g].rearrange("q s j -> q (s j)"),
                 )
 
-            if q % QUADS_PER_CLIP == 0:
-                for which in ("t", "p"):
-                    tp_grouped[which] = keep.tile(
-                        [P, L, PACK], BF16, align_bytes=64, name="grouped_%s%d" % (which, clip)
-                    )
-                    tp_codes[which] = keep.tile([P, L], U32, align_bytes=64, name="codes_%s%d" % (which, clip))
-                    tp_scales[which] = keep.tile([P, L], U8, align_bytes=64, name="scales_%s%d" % (which, clip))
-
-            for h in range(CHUNKS_PER_QUAD):
-                in_quad = slice(h * CHUNK, (h + 1) * CHUNK)
-                first = (q % QUADS_PER_CLIP) * QUAD + h * CHUNK
-                in_clip = slice(first, first + CHUNK)
-                for which in ("t", "p"):
-                    acc = psum_tp.tile([P, FEATURE_TILES, CHUNK], F32, name="acc")
-                    for m in range(FEATURE_TILES):
-                        for g in range(C_PASSES):
-                            nc.tensor.matmul_mx(
-                                out=acc[:, m, :],
-                                lhsT=w_codes[which][:, m, g, :].bitcast(FP8X4),
-                                lhsT_scale=w_scales[which][:, m, g, :],
-                                rhs=x_codes[:, g, in_quad].bitcast(FP8X4),
-                                rhs_scale=x_scales[:, g, in_quad],
-                                start=(g == 0),
-                                stop=(g == C_PASSES - 1),
-                            )
-                    nc.vector.tensor_tensor(
-                        out=tp_grouped[which][:, in_clip, :],
-                        in0=acc[:].rearrange("p m r -> p r m"),
-                        in1=bias[which][:].unsqueeze(1).to_broadcast([P, CHUNK, FEATURE_TILES]),
-                        op=ADD,
-                    )
-                for which in ("t", "p"):
-                    nc.vector.quantize_mx(
-                        out=tp_codes[which][:, in_clip].bitcast(FP8X4),
-                        scales=tp_scales[which][:, in_clip],
-                        in_=tp_grouped[which][:, in_clip, :].rearrange("p r m -> p (r m)"),
-                    )
-
-            if q % QUADS_PER_CLIP == QUADS_PER_CLIP - 1:
-                for i in range(ROW_TILES):
-                    rows = slice(i * P, (i + 1) * P)
-                    affinity = psum_out.tile([P, L], F32, name="affinity")
+        def project(which, clip, chunk):
+            quad = clip * QUADS_PER_CLIP + chunk // CHUNKS_PER_QUAD
+            first = (chunk % CHUNKS_PER_QUAD) * CHUNK
+            positions = slice(first, first + CHUNK)
+            acc[which, clip, chunk] = psum_tp.tile([P, FEATURE_TILES, CHUNK], F32, name="acc")
+            for m in range(FEATURE_TILES):
+                for g in range(C_PASSES):
                     nc.tensor.matmul_mx(
-                        out=affinity[:],
-                        lhsT=tp_codes["t"][:, rows].bitcast(FP8X4),
-                        lhsT_scale=tp_scales["t"][:, rows],
-                        rhs=tp_codes["p"][:].bitcast(FP8X4),
-                        rhs_scale=tp_scales["p"][:],
-                        start=True,
-                        stop=True,
+                        out=acc[which, clip, chunk][:, m, :],
+                        lhsT=w_codes[which][:, m, g, :].bitcast(FP8X4),
+                        lhsT_scale=w_scales[which][:, m, g, :],
+                        rhs=x_codes[quad][:, g, positions].bitcast(FP8X4),
+                        rhs_scale=x_scales[quad][:, g, positions],
+                        start=(g == 0),
+                        stop=(g == C_PASSES - 1),
                     )
-                    result = keep.tile([P, L], F32, name="result_%d_%d" % (clip, i))
-                    nc.scalar.copy(out=result[:], in_=affinity[:])
-                    nc.sync.dma_start(out=out[clip, rows, :], in_=result[:])
+
+        def finish(which, clip, chunk):
+            if chunk == 0:
+                tp_grouped[which] = keep.tile(
+                    [P, L, PACK], BF16, align_bytes=64, name="grouped_%s%d" % (which, clip)
+                )
+                tp_codes[which] = keep.tile([P, L], U32, align_bytes=64, name="codes_%s%d" % (which, clip))
+                tp_scales[which] = keep.tile([P, L], U8, align_bytes=64, name="scales_%s%d" % (which, clip))
+            positions = slice(chunk * CHUNK, (chunk + 1) * CHUNK)
+            nc.vector.tensor_tensor(
+                out=tp_grouped[which][:, positions, :],
+                in0=acc[which, clip, chunk][:].rearrange("n m r -> n r m"),
+                in1=bias[which][:].unsqueeze(1).to_broadcast([P, CHUNK, FEATURE_TILES]),
+                op=ADD,
+            )
+            nc.vector.quantize_mx(
+                out=tp_codes[which][:, positions].bitcast(FP8X4),
+                scales=tp_scales[which][:, positions],
+                in_=tp_grouped[which][:, positions, :].rearrange("n r m -> n (r m)"),
+            )
+
+        def affinity_rows(clip, chunk):
+            rows = slice(chunk * CHUNK, (chunk + 1) * CHUNK)
+            affinity = psum_wide.tile([P, L], F32, name="affinity", tag="wide")
+            nc.tensor.matmul_mx(
+                out=affinity[:],
+                lhsT=tp_codes["t"][:, rows].bitcast(FP8X4),
+                lhsT_scale=tp_scales["t"][:, rows],
+                rhs=tp_codes["p"][:].bitcast(FP8X4),
+                rhs_scale=tp_scales["p"][:],
+                start=True,
+                stop=True,
+            )
+            result = keep.tile([P, L], F32, name="result_%d_%d" % (clip, chunk))
+            nc.scalar.copy(out=result[:], in_=affinity[:])
+            nc.sync.dma_start(out=out[clip, rows, :], in_=result[:])
+
+        load_weight("p", p_w, p_b)
+        load_x(0)
+        load_x(1)
+        load_weight("t", t_w, t_b)
+        load_x(2)
+        load_x(3)
+
+        prepare_weight("p")
+        prepare_x(0, nc.vector.tensor_copy)
+        prepare_x(1, nc.scalar.copy)
+        for chunk in range(CHUNKS):
+            project("p", 0, chunk)
+        prepare_weight("t")
+        for chunk in range(CHUNKS):
+            finish("p", 0, chunk)
+            project("t", 0, chunk)
+        prepare_x(2, nc.scalar.copy)
+        prepare_x(3, nc.scalar.copy)
+        for chunk in range(CHUNKS):
+            finish("t", 0, chunk)
+            affinity_rows(0, chunk)
+            project("p", 1, chunk)
+        for chunk in range(CHUNKS):
+            finish("p", 1, chunk)
+            project("t", 1, chunk)
+        for chunk in range(CHUNKS):
+            finish("t", 1, chunk)
+            affinity_rows(1, chunk)

@@ -28,6 +28,7 @@ QUADS_PER_CLIP = L // QUAD
 CHUNK = 128
 CHUNKS = L // CHUNK
 CHUNKS_PER_QUAD = QUAD // CHUNK
+AHEAD = 4
 
 FLOPS = 2 * 2 * CLIPS * L * C * FEATURES + 2 * CLIPS * L * L * FEATURES
 
@@ -37,7 +38,7 @@ def tile_stnonlocalgnlstage_pa_kernel(tc, x, t_w, t_b, p_w, p_b, out):
     with ExitStack() as stack:
         keep = stack.enter_context(tc.tile_pool(name="keep", bufs=1))
         psum_wide = stack.enter_context(tc.psum_pool(name="psum_wide", bufs=4))
-        psum_tp = stack.enter_context(tc.psum_pool(name="psum_tp", bufs=4))
+        psum_tp = stack.enter_context(tc.psum_pool(name="psum_tp", bufs=AHEAD))
 
         identity = keep.tile([P, P], F32, name="identity")
         make_identity(nc, identity[:])
@@ -128,24 +129,27 @@ def tile_stnonlocalgnlstage_pa_kernel(tc, x, t_w, t_b, p_w, p_b, out):
                         stop=(g == C_PASSES - 1),
                     )
 
-        def finish(which, clip, chunk):
+        def add_bias(which, clip, chunk):
             if chunk == 0:
-                tp_grouped[which] = keep.tile(
+                tp_grouped[which, clip] = keep.tile(
                     [P, L, PACK], BF16, align_bytes=64, name="grouped_%s%d" % (which, clip)
                 )
-                tp_codes[which] = keep.tile([P, L], U32, align_bytes=64, name="codes_%s%d" % (which, clip))
-                tp_scales[which] = keep.tile([P, L], U8, align_bytes=64, name="scales_%s%d" % (which, clip))
+                tp_codes[which, clip] = keep.tile([P, L], U32, align_bytes=64, name="codes_%s%d" % (which, clip))
+                tp_scales[which, clip] = keep.tile([P, L], U8, align_bytes=64, name="scales_%s%d" % (which, clip))
             positions = slice(chunk * CHUNK, (chunk + 1) * CHUNK)
             nc.vector.tensor_tensor(
-                out=tp_grouped[which][:, positions, :],
+                out=tp_grouped[which, clip][:, positions, :],
                 in0=acc[which, clip, chunk][:].rearrange("n m r -> n r m"),
                 in1=bias[which][:].unsqueeze(1).to_broadcast([P, CHUNK, FEATURE_TILES]),
                 op=ADD,
             )
+
+        def quantise_tp(which, clip, chunk):
+            positions = slice(chunk * CHUNK, (chunk + 1) * CHUNK)
             nc.vector.quantize_mx(
-                out=tp_codes[which][:, positions].bitcast(FP8X4),
-                scales=tp_scales[which][:, positions],
-                in_=tp_grouped[which][:, positions, :].rearrange("n r m -> n (r m)"),
+                out=tp_codes[which, clip][:, positions].bitcast(FP8X4),
+                scales=tp_scales[which, clip][:, positions],
+                in_=tp_grouped[which, clip][:, positions, :].rearrange("n r m -> n (r m)"),
             )
 
         def affinity_rows(clip, chunk):
@@ -153,10 +157,10 @@ def tile_stnonlocalgnlstage_pa_kernel(tc, x, t_w, t_b, p_w, p_b, out):
             affinity = psum_wide.tile([P, L], F32, name="affinity", tag="wide")
             nc.tensor.matmul_mx(
                 out=affinity[:],
-                lhsT=tp_codes["t"][:, rows].bitcast(FP8X4),
-                lhsT_scale=tp_scales["t"][:, rows],
-                rhs=tp_codes["p"][:].bitcast(FP8X4),
-                rhs_scale=tp_scales["p"][:],
+                lhsT=tp_codes["t", clip][:, rows].bitcast(FP8X4),
+                lhsT_scale=tp_scales["t", clip][:, rows],
+                rhs=tp_codes["p", clip][:].bitcast(FP8X4),
+                rhs_scale=tp_scales["p", clip][:],
                 start=True,
                 stop=True,
             )
@@ -171,24 +175,23 @@ def tile_stnonlocalgnlstage_pa_kernel(tc, x, t_w, t_b, p_w, p_b, out):
         load_x(2)
         load_x(3)
 
-        prepare_weight("p")
-        prepare_x(0, nc.vector.tensor_copy)
-        prepare_x(1, nc.scalar.copy)
-        for chunk in range(CHUNKS):
-            project("p", 0, chunk)
-        prepare_weight("t")
-        for chunk in range(CHUNKS):
-            finish("p", 0, chunk)
-            project("t", 0, chunk)
-        prepare_x(2, nc.scalar.copy)
-        prepare_x(3, nc.scalar.copy)
-        for chunk in range(CHUNKS):
-            finish("t", 0, chunk)
-            affinity_rows(0, chunk)
-            project("p", 1, chunk)
-        for chunk in range(CHUNKS):
-            finish("p", 1, chunk)
-            project("t", 1, chunk)
-        for chunk in range(CHUNKS):
-            finish("t", 1, chunk)
-            affinity_rows(1, chunk)
+        units = [
+            (which, clip, chunk) for clip in range(CLIPS) for which in ("p", "t") for chunk in range(CHUNKS)
+        ]
+        for step in range(len(units) + AHEAD + 1):
+            if 0 <= step - AHEAD < len(units):
+                which, clip, chunk = units[step - AHEAD]
+                add_bias(which, clip, chunk)
+            if 0 <= step - AHEAD - 1:
+                which, clip, chunk = units[step - AHEAD - 1]
+                quantise_tp(which, clip, chunk)
+                if which == "t":
+                    affinity_rows(clip, chunk)
+            if step < len(units):
+                which, clip, chunk = units[step]
+                if clip == 0 and chunk == 0:
+                    prepare_weight(which)
+                if which == "p" and chunk % CHUNKS_PER_QUAD == 0:
+                    quad = clip * QUADS_PER_CLIP + chunk // CHUNKS_PER_QUAD
+                    prepare_x(quad, nc.vector.tensor_copy if quad == 0 else nc.scalar.copy)
+                project(which, clip, chunk)

@@ -28,7 +28,9 @@ QUADS_PER_CLIP = L // QUAD
 CHUNK = 128
 CHUNKS = L // CHUNK
 CHUNKS_PER_QUAD = QUAD // CHUNK
-AHEAD = 4
+QUADS = CLIPS * QUADS_PER_CLIP
+TP_BANKS = 4
+AHEAD = 3
 
 FLOPS = 2 * 2 * CLIPS * L * C * FEATURES + 2 * CLIPS * L * L * FEATURES
 
@@ -38,13 +40,14 @@ def tile_stnonlocalgnlstage_pa_kernel(tc, x, t_w, t_b, p_w, p_b, out):
     with ExitStack() as stack:
         keep = stack.enter_context(tc.tile_pool(name="keep", bufs=1))
         psum_wide = stack.enter_context(tc.psum_pool(name="psum_wide", bufs=4))
-        psum_tp = stack.enter_context(tc.psum_pool(name="psum_tp", bufs=AHEAD))
+        psum_tp = stack.enter_context(tc.psum_pool(name="psum_tp", bufs=TP_BANKS))
+        stack.enter_context(tc.manual_schedule())
 
         identity = keep.tile([P, P], F32, name="identity")
         make_identity(nc, identity[:])
 
-        w_raw, bias, w_codes, w_scales = {}, {}, {}, {}
-        x_raw, x_codes, x_scales = {}, {}, {}
+        w_raw, bias, w_grouped, w_codes, w_scales = {}, {}, {}, {}, {}
+        x_raw, x_grouped, x_codes, x_scales = {}, {}, {}, {}
         acc, tp_grouped, tp_codes, tp_scales = {}, {}, {}, {}
 
         def load_weight(which, w, b):
@@ -66,15 +69,9 @@ def tile_stnonlocalgnlstage_pa_kernel(tc, x, t_w, t_b, p_w, p_b, out):
                     in_=x[frames, channels].rearrange("f (q j) h w -> q f (j h w)", j=PACK),
                 )
 
-        def prepare_weight(which):
+        def group_weight(which):
             words = w_raw[which][:].bitcast(F32).rearrange(
                 "n (m g q u) -> n m g u q", m=FEATURE_TILES, g=C_PASSES, u=2
-            )
-            w_codes[which] = keep.tile(
-                [P, FEATURE_TILES, C_PASSES, P], U32, align_bytes=64, name="w_codes_%s" % which
-            )
-            w_scales[which] = keep.tile(
-                [P, FEATURE_TILES, C_PASSES, P], U8, align_bytes=64, name="w_scales_%s" % which
             )
             for m in range(FEATURE_TILES):
                 flipped = psum_wide.tile([P, C_PASSES, 2, P], F32, name="flipped", tag="wide")
@@ -83,33 +80,46 @@ def tile_stnonlocalgnlstage_pa_kernel(tc, x, t_w, t_b, p_w, p_b, out):
                         nc.tensor.transpose(
                             out=flipped[:, g, u, :], in_=words[:, m, g, u, :], identity=identity[:]
                         )
-                w_grouped = keep.tile(
+                w_grouped[which, m] = keep.tile(
                     [P, C_PASSES * P * PACK], BF16, align_bytes=64, name="w_grouped_%s%d" % (which, m)
                 )
                 nc.scalar.copy(
-                    out=w_grouped[:].bitcast(F32).rearrange("q (g n u) -> q g n u", g=C_PASSES, u=2),
+                    out=w_grouped[which, m][:].bitcast(F32).rearrange("q (g n u) -> q g n u", g=C_PASSES, u=2),
                     in_=flipped[:].rearrange("q g u n -> q g n u"),
                 )
+
+        def quantise_weight(which):
+            w_codes[which] = keep.tile(
+                [P, FEATURE_TILES, C_PASSES, P], U32, align_bytes=64, name="w_codes_%s" % which
+            )
+            w_scales[which] = keep.tile(
+                [P, FEATURE_TILES, C_PASSES, P], U8, align_bytes=64, name="w_scales_%s" % which
+            )
+            for m in range(FEATURE_TILES):
                 nc.vector.quantize_mx(
                     out=w_codes[which][:, m].rearrange("q g n -> q (g n)").bitcast(FP8X4),
                     scales=w_scales[which][:, m].rearrange("q g n -> q (g n)"),
-                    in_=w_grouped[:],
+                    in_=w_grouped[which, m][:],
                 )
 
-        def prepare_x(quad, copy):
-            x_grouped = keep.tile([P, C_PASSES, QUAD, PACK], BF16, align_bytes=64, name="x_grouped_%d" % quad)
-            x_codes[quad] = keep.tile([P, C_PASSES, QUAD], U32, align_bytes=64, name="x_codes_%d" % quad)
-            x_scales[quad] = keep.tile([P, C_PASSES, QUAD], U8, align_bytes=64, name="x_scales_%d" % quad)
+        def group_x(quad, copy):
+            x_grouped[quad] = keep.tile(
+                [P, C_PASSES, QUAD, PACK], BF16, align_bytes=64, name="x_grouped_%d" % quad
+            )
             for g in range(C_PASSES):
                 copy(
-                    out=x_grouped[:, g].rearrange("q (f s) j -> q f s j", f=QUAD_FRAMES),
+                    out=x_grouped[quad][:, g].rearrange("q (f s) j -> q f s j", f=QUAD_FRAMES),
                     in_=x_raw[quad][:, g].rearrange("q f (j s) -> q f s j", j=PACK),
                 )
+
+        def quantise_x(quad):
+            x_codes[quad] = keep.tile([P, C_PASSES, QUAD], U32, align_bytes=64, name="x_codes_%d" % quad)
+            x_scales[quad] = keep.tile([P, C_PASSES, QUAD], U8, align_bytes=64, name="x_scales_%d" % quad)
             for g in range(C_PASSES):
                 nc.vector.quantize_mx(
                     out=x_codes[quad][:, g].bitcast(FP8X4),
                     scales=x_scales[quad][:, g],
-                    in_=x_grouped[:, g].rearrange("q s j -> q (s j)"),
+                    in_=x_grouped[quad][:, g].rearrange("q s j -> q (s j)"),
                 )
 
         def project(which, clip, chunk):
@@ -170,28 +180,45 @@ def tile_stnonlocalgnlstage_pa_kernel(tc, x, t_w, t_b, p_w, p_b, out):
 
         load_weight("p", p_w, p_b)
         load_x(0)
-        load_x(1)
         load_weight("t", t_w, t_b)
-        load_x(2)
-        load_x(3)
+        for quad in range(1, QUADS):
+            load_x(quad)
+
+        group_weight("p")
+        quantise_weight("p")
+        group_x(0, nc.vector.tensor_copy)
+        quantise_x(0)
+        group_weight("t")
+        for quad in range(1, QUADS):
+            group_x(quad, nc.scalar.copy)
 
         units = [
-            (which, clip, chunk) for clip in range(CLIPS) for which in ("p", "t") for chunk in range(CHUNKS)
+            (which, quad // QUADS_PER_CLIP, (quad % QUADS_PER_CLIP) * CHUNKS_PER_QUAD + half)
+            for quad in range(QUADS)
+            for which in ("p", "t")
+            for half in range(CHUNKS_PER_QUAD)
         ]
-        for step in range(len(units) + AHEAD + 1):
-            if 0 <= step - AHEAD < len(units):
-                which, clip, chunk = units[step - AHEAD]
-                add_bias(which, clip, chunk)
-            if 0 <= step - AHEAD - 1:
-                which, clip, chunk = units[step - AHEAD - 1]
+
+        def start(which, clip, chunk):
+            quad = clip * QUADS_PER_CLIP + chunk // CHUNKS_PER_QUAD
+            if (which, quad, chunk) == ("t", 0, 0):
+                quantise_weight("t")
+            if which == "p" and chunk % CHUNKS_PER_QUAD == 0 and quad > 0:
+                quantise_x(quad)
+            project(which, clip, chunk)
+
+        for unit in units[:AHEAD]:
+            start(*unit)
+        for i in range(len(units) + 1):
+            if i < len(units):
+                add_bias(*units[i])
+            if i > 0:
+                which, clip, chunk = units[i - 1]
                 quantise_tp(which, clip, chunk)
-                if which == "t":
+                if which == "p" and chunk == CHUNKS - 1:
+                    for early in range(CHUNKS_PER_QUAD):
+                        affinity_rows(clip, early)
+                if which == "t" and chunk >= CHUNKS_PER_QUAD:
                     affinity_rows(clip, chunk)
-            if step < len(units):
-                which, clip, chunk = units[step]
-                if clip == 0 and chunk == 0:
-                    prepare_weight(which)
-                if which == "p" and chunk % CHUNKS_PER_QUAD == 0:
-                    quad = clip * QUADS_PER_CLIP + chunk // CHUNKS_PER_QUAD
-                    prepare_x(quad, nc.vector.tensor_copy if quad == 0 else nc.scalar.copy)
-                project(which, clip, chunk)
+            if i + AHEAD < len(units):
+                start(*units[i + AHEAD])

@@ -22,13 +22,11 @@ C_PASSES = C // K_PASS
 FEATURES = 512
 FEATURE_TILES = FEATURES // P
 
-QUAD_FRAMES = 4
-QUAD = QUAD_FRAMES * GRID
-QUADS_PER_CLIP = L // QUAD
 CHUNK = 128
 CHUNKS = L // CHUNK
-CHUNKS_PER_QUAD = QUAD // CHUNK
-QUADS = CLIPS * QUADS_PER_CLIP
+CHUNK_FRAMES = CHUNK // GRID
+LOAD_CHUNKS = 2
+LOADS_PER_CLIP = CHUNKS // LOAD_CHUNKS
 TP_BANKS = 4
 AHEAD = 3
 
@@ -59,14 +57,17 @@ def tile_stnonlocalgnlstage_pa_kernel(tc, x, t_w, t_b, p_w, p_b, out):
             bias[which] = keep.tile([P, FEATURE_TILES], BF16, name="bias_%s" % which)
             nc.scalar.dma_start(out=bias[which][:], in_=b.rearrange("(n m) -> n m", m=FEATURE_TILES))
 
-        def load_x(quad):
-            x_raw[quad] = keep.tile([P, C_PASSES, QUAD_FRAMES, PACK * GRID], BF16, name="x_raw_%d" % quad)
-            frames = slice(quad * QUAD_FRAMES, (quad + 1) * QUAD_FRAMES)
+        def load_x(clip, piece):
+            n_frames = LOAD_CHUNKS * CHUNK_FRAMES
+            x_raw[clip, piece] = keep.tile(
+                [P, C_PASSES, n_frames, PACK * GRID], BF16, name="x_raw_%d_%d" % (clip, piece)
+            )
+            first = (clip * LOADS_PER_CLIP + piece) * n_frames
             for g in range(C_PASSES):
                 channels = slice(g * K_PASS, (g + 1) * K_PASS)
                 nc.sync.dma_start(
-                    out=x_raw[quad][:, g],
-                    in_=x[frames, channels].rearrange("f (q j) h w -> q f (j h w)", j=PACK),
+                    out=x_raw[clip, piece][:, g],
+                    in_=x[first : first + n_frames, channels].rearrange("f (q j) h w -> q f (j h w)", j=PACK),
                 )
 
         def group_weight(which):
@@ -102,30 +103,32 @@ def tile_stnonlocalgnlstage_pa_kernel(tc, x, t_w, t_b, p_w, p_b, out):
                     in_=w_grouped[which, m][:],
                 )
 
-        def group_x(quad, copy):
-            x_grouped[quad] = keep.tile(
-                [P, C_PASSES, QUAD, PACK], BF16, align_bytes=64, name="x_grouped_%d" % quad
+        def group_x(clip, chunk, copy):
+            x_grouped[clip, chunk] = keep.tile(
+                [P, C_PASSES, CHUNK, PACK], BF16, align_bytes=64, name="x_grouped_%d_%d" % (clip, chunk)
             )
+            first = (chunk % LOAD_CHUNKS) * CHUNK_FRAMES
+            frames = slice(first, first + CHUNK_FRAMES)
             for g in range(C_PASSES):
                 copy(
-                    out=x_grouped[quad][:, g].rearrange("q (f s) j -> q f s j", f=QUAD_FRAMES),
-                    in_=x_raw[quad][:, g].rearrange("q f (j s) -> q f s j", j=PACK),
+                    out=x_grouped[clip, chunk][:, g].rearrange("q (f s) j -> q f s j", f=CHUNK_FRAMES),
+                    in_=x_raw[clip, chunk // LOAD_CHUNKS][:, g, frames].rearrange("q f (j s) -> q f s j", j=PACK),
                 )
 
-        def quantise_x(quad):
-            x_codes[quad] = keep.tile([P, C_PASSES, QUAD], U32, align_bytes=64, name="x_codes_%d" % quad)
-            x_scales[quad] = keep.tile([P, C_PASSES, QUAD], U8, align_bytes=64, name="x_scales_%d" % quad)
-            for g in range(C_PASSES):
-                nc.vector.quantize_mx(
-                    out=x_codes[quad][:, g].bitcast(FP8X4),
-                    scales=x_scales[quad][:, g],
-                    in_=x_grouped[quad][:, g].rearrange("q s j -> q (s j)"),
-                )
+        def quantise_x(clip, chunk):
+            x_codes[clip, chunk] = keep.tile(
+                [P, C_PASSES, CHUNK], U32, align_bytes=64, name="x_codes_%d_%d" % (clip, chunk)
+            )
+            x_scales[clip, chunk] = keep.tile(
+                [P, C_PASSES, CHUNK], U8, align_bytes=64, name="x_scales_%d_%d" % (clip, chunk)
+            )
+            nc.vector.quantize_mx(
+                out=x_codes[clip, chunk][:].rearrange("q g s -> q (g s)").bitcast(FP8X4),
+                scales=x_scales[clip, chunk][:].rearrange("q g s -> q (g s)"),
+                in_=x_grouped[clip, chunk][:].rearrange("q g s j -> q (g s j)"),
+            )
 
         def project(which, clip, chunk):
-            quad = clip * QUADS_PER_CLIP + chunk // CHUNKS_PER_QUAD
-            first = (chunk % CHUNKS_PER_QUAD) * CHUNK
-            positions = slice(first, first + CHUNK)
             acc[which, clip, chunk] = psum_tp.tile([P, FEATURE_TILES, CHUNK], F32, name="acc")
             for m in range(FEATURE_TILES):
                 for g in range(C_PASSES):
@@ -133,8 +136,8 @@ def tile_stnonlocalgnlstage_pa_kernel(tc, x, t_w, t_b, p_w, p_b, out):
                         out=acc[which, clip, chunk][:, m, :],
                         lhsT=w_codes[which][:, m, g, :].bitcast(FP8X4),
                         lhsT_scale=w_scales[which][:, m, g, :],
-                        rhs=x_codes[quad][:, g, positions].bitcast(FP8X4),
-                        rhs_scale=x_scales[quad][:, g, positions],
+                        rhs=x_codes[clip, chunk][:, g, :].bitcast(FP8X4),
+                        rhs_scale=x_scales[clip, chunk][:, g, :],
                         start=(g == 0),
                         stop=(g == C_PASSES - 1),
                     )
@@ -179,34 +182,38 @@ def tile_stnonlocalgnlstage_pa_kernel(tc, x, t_w, t_b, p_w, p_b, out):
             nc.sync.dma_start(out=out[clip, rows, :], in_=result[:])
 
         load_weight("p", p_w, p_b)
-        load_x(0)
+        load_x(0, 0)
         load_weight("t", t_w, t_b)
-        for quad in range(1, QUADS):
-            load_x(quad)
+        load_x(0, 1)
+        for piece in range(LOADS_PER_CLIP):
+            load_x(1, piece)
 
         group_weight("p")
         quantise_weight("p")
-        group_x(0, nc.vector.tensor_copy)
-        quantise_x(0)
+        for chunk in range(LOAD_CHUNKS):
+            group_x(0, chunk, nc.vector.tensor_copy)
         group_weight("t")
-        for quad in range(1, QUADS):
-            group_x(quad, nc.scalar.copy)
+        for chunk in range(LOAD_CHUNKS, CHUNKS):
+            group_x(0, chunk, nc.scalar.copy)
+        for chunk in range(CHUNKS):
+            group_x(1, chunk, nc.scalar.copy)
 
         units = [
-            (which, quad // QUADS_PER_CLIP, (quad % QUADS_PER_CLIP) * CHUNKS_PER_QUAD + half)
-            for quad in range(QUADS)
+            (which, 0, piece * LOAD_CHUNKS + k)
+            for piece in range(LOADS_PER_CLIP)
             for which in ("p", "t")
-            for half in range(CHUNKS_PER_QUAD)
-        ]
+            for k in range(LOAD_CHUNKS)
+        ] + [(which, 1, chunk) for which in ("p", "t") for chunk in range(CHUNKS)]
 
         def start(which, clip, chunk):
-            quad = clip * QUADS_PER_CLIP + chunk // CHUNKS_PER_QUAD
-            if (which, quad, chunk) == ("t", 0, 0):
+            if (which, clip, chunk) == ("t", 0, 0):
                 quantise_weight("t")
-            if which == "p" and chunk % CHUNKS_PER_QUAD == 0 and quad > 0:
-                quantise_x(quad)
+            if which == "p":
+                quantise_x(clip, chunk)
             project(which, clip, chunk)
 
+        quantised = set()
+        multiplied = set()
         for unit in units[:AHEAD]:
             start(*unit)
         for i in range(len(units) + 1):
@@ -215,10 +222,11 @@ def tile_stnonlocalgnlstage_pa_kernel(tc, x, t_w, t_b, p_w, p_b, out):
             if i > 0:
                 which, clip, chunk = units[i - 1]
                 quantise_tp(which, clip, chunk)
-                if which == "p" and chunk == CHUNKS - 1:
-                    for early in range(CHUNKS_PER_QUAD):
-                        affinity_rows(clip, early)
-                if which == "t" and chunk >= CHUNKS_PER_QUAD:
-                    affinity_rows(clip, chunk)
+                quantised.add(units[i - 1])
+                if all([("p", clip, c) in quantised for c in range(CHUNKS)]):
+                    for c in range(CHUNKS):
+                        if ("t", clip, c) in quantised and (clip, c) not in multiplied:
+                            affinity_rows(clip, c)
+                            multiplied.add((clip, c))
             if i + AHEAD < len(units):
                 start(*units[i + AHEAD])

@@ -28,6 +28,7 @@ CHUNK_FRAMES = CHUNK // GRID
 LOAD_CHUNKS = 2
 LOADS_PER_CLIP = CHUNKS // LOAD_CHUNKS
 TP_BANKS = 4
+RUN = 4
 AHEAD = 3
 
 FLOPS = 2 * 2 * CLIPS * L * C * FEATURES + 2 * CLIPS * L * L * FEATURES
@@ -108,12 +109,16 @@ def tile_stnonlocalgnlstage_pa_kernel(tc, x, t_w, t_b, p_w, p_b, out):
                 [P, C_PASSES, CHUNK, PACK], BF16, align_bytes=64, name="x_grouped_%d_%d" % (clip, chunk)
             )
             first = (chunk % LOAD_CHUNKS) * CHUNK_FRAMES
-            frames = slice(first, first + CHUNK_FRAMES)
             for g in range(C_PASSES):
-                copy(
-                    out=x_grouped[clip, chunk][:, g].rearrange("q (f s) j -> q f s j", f=CHUNK_FRAMES),
-                    in_=x_raw[clip, chunk // LOAD_CHUNKS][:, g, frames].rearrange("q f (j s) -> q f s j", j=PACK),
-                )
+                for f in range(CHUNK_FRAMES):
+                    copy(
+                        out=x_grouped[clip, chunk][:, g, f * GRID : (f + 1) * GRID, :].rearrange(
+                            "q (c i) j -> q c j i", i=RUN
+                        ),
+                        in_=x_raw[clip, chunk // LOAD_CHUNKS][:, g, first + f].rearrange(
+                            "q (j c i) -> q c j i", j=PACK, i=RUN
+                        ),
+                    )
 
         def quantise_x(clip, chunk):
             x_codes[clip, chunk] = keep.tile(

@@ -25,8 +25,6 @@ FEATURE_TILES = FEATURES // P
 CHUNK = 128
 CHUNKS = L // CHUNK
 CHUNK_FRAMES = CHUNK // GRID
-LOAD_CHUNKS = 2
-LOADS_PER_CLIP = CHUNKS // LOAD_CHUNKS
 TP_BANKS = 4
 RUN = 4
 AHEAD = 3
@@ -58,18 +56,17 @@ def tile_stnonlocalgnlstage_pa_kernel(tc, x, t_w, t_b, p_w, p_b, out):
             bias[which] = keep.tile([P, FEATURE_TILES], BF16, name="bias_%s" % which)
             nc.scalar.dma_start(out=bias[which][:], in_=b.rearrange("(n m) -> n m", m=FEATURE_TILES))
 
-        def load_x(clip, piece):
-            n_frames = LOAD_CHUNKS * CHUNK_FRAMES
-            x_raw[clip, piece] = keep.tile(
-                [P, C_PASSES, n_frames, PACK * GRID], BF16, name="x_raw_%d_%d" % (clip, piece)
+        def load_x(clip, chunk):
+            x_raw[clip, chunk] = keep.tile(
+                [P, CHUNK_FRAMES, C_PASSES, PACK * GRID], BF16, name="x_raw_%d_%d" % (clip, chunk)
             )
-            first = (clip * LOADS_PER_CLIP + piece) * n_frames
-            for g in range(C_PASSES):
-                channels = slice(g * K_PASS, (g + 1) * K_PASS)
-                nc.sync.dma_start(
-                    out=x_raw[clip, piece][:, g],
-                    in_=x[first : first + n_frames, channels].rearrange("f (q j) h w -> q f (j h w)", j=PACK),
-                )
+            first = (clip * CHUNKS + chunk) * CHUNK_FRAMES
+            nc.sync.dma_start(
+                out=x_raw[clip, chunk][:].rearrange("q f g r -> q (f g) r"),
+                in_=x[first : first + CHUNK_FRAMES].rearrange(
+                    "f (g q j) h w -> q (f g) (j h w)", g=C_PASSES, j=PACK
+                ),
+            )
 
         def group_weight(which):
             words = w_raw[which][:].bitcast(F32).rearrange(
@@ -90,32 +87,31 @@ def tile_stnonlocalgnlstage_pa_kernel(tc, x, t_w, t_b, p_w, p_b, out):
                     in_=flipped[:].rearrange("q g u n -> q g n u"),
                 )
 
-        def quantise_weight(which):
-            w_codes[which] = keep.tile(
-                [P, FEATURE_TILES, C_PASSES, P], U32, align_bytes=64, name="w_codes_%s" % which
-            )
-            w_scales[which] = keep.tile(
-                [P, FEATURE_TILES, C_PASSES, P], U8, align_bytes=64, name="w_scales_%s" % which
-            )
-            for m in range(FEATURE_TILES):
-                nc.vector.quantize_mx(
-                    out=w_codes[which][:, m].rearrange("q g n -> q (g n)").bitcast(FP8X4),
-                    scales=w_scales[which][:, m].rearrange("q g n -> q (g n)"),
-                    in_=w_grouped[which, m][:],
+        def quantise_weight(which, m):
+            if m == 0:
+                w_codes[which] = keep.tile(
+                    [P, FEATURE_TILES, C_PASSES, P], U32, align_bytes=64, name="w_codes_%s" % which
                 )
+                w_scales[which] = keep.tile(
+                    [P, FEATURE_TILES, C_PASSES, P], U8, align_bytes=64, name="w_scales_%s" % which
+                )
+            nc.vector.quantize_mx(
+                out=w_codes[which][:, m].rearrange("q g n -> q (g n)").bitcast(FP8X4),
+                scales=w_scales[which][:, m].rearrange("q g n -> q (g n)"),
+                in_=w_grouped[which, m][:],
+            )
 
         def group_x(clip, chunk, copy):
             x_grouped[clip, chunk] = keep.tile(
                 [P, C_PASSES, CHUNK, PACK], BF16, align_bytes=64, name="x_grouped_%d_%d" % (clip, chunk)
             )
-            first = (chunk % LOAD_CHUNKS) * CHUNK_FRAMES
             for g in range(C_PASSES):
                 for f in range(CHUNK_FRAMES):
                     copy(
                         out=x_grouped[clip, chunk][:, g, f * GRID : (f + 1) * GRID, :].rearrange(
                             "q (c i) j -> q c j i", i=RUN
                         ),
-                        in_=x_raw[clip, chunk // LOAD_CHUNKS][:, g, first + f].rearrange(
+                        in_=x_raw[clip, chunk][:, f, g].rearrange(
                             "q (j c i) -> q c j i", j=PACK, i=RUN
                         ),
                     )
@@ -170,57 +166,67 @@ def tile_stnonlocalgnlstage_pa_kernel(tc, x, t_w, t_b, p_w, p_b, out):
                 in_=tp_grouped[which, clip][:, positions, :].rearrange("n r m -> n (r m)"),
             )
 
-        def affinity_rows(clip, chunk):
+        def affinity_rows(clip, chunk, pieces):
             rows = slice(chunk * CHUNK, (chunk + 1) * CHUNK)
-            affinity = psum_wide.tile([P, L], F32, name="affinity", tag="wide")
-            nc.tensor.matmul_mx(
-                out=affinity[:],
-                lhsT=tp_codes["t", clip][:, rows].bitcast(FP8X4),
-                lhsT_scale=tp_scales["t", clip][:, rows],
-                rhs=tp_codes["p", clip][:].bitcast(FP8X4),
-                rhs_scale=tp_scales["p", clip][:],
-                start=True,
-                stop=True,
-            )
-            result = keep.tile([P, L], F32, name="result_%d_%d" % (clip, chunk))
-            nc.scalar.copy(out=result[:], in_=affinity[:])
-            nc.sync.dma_start(out=out[clip, rows, :], in_=result[:])
+            width = L // pieces
+            for piece in range(pieces):
+                cols = slice(piece * width, (piece + 1) * width)
+                affinity = psum_wide.tile([P, width], F32, name="affinity", tag="wide")
+                nc.tensor.matmul_mx(
+                    out=affinity[:],
+                    lhsT=tp_codes["t", clip][:, rows].bitcast(FP8X4),
+                    lhsT_scale=tp_scales["t", clip][:, rows],
+                    rhs=tp_codes["p", clip][:, cols].bitcast(FP8X4),
+                    rhs_scale=tp_scales["p", clip][:, cols],
+                    start=True,
+                    stop=True,
+                )
+                result = keep.tile([P, width], F32, name="result_%d_%d_%d" % (clip, chunk, piece))
+                nc.scalar.copy(out=result[:], in_=affinity[:])
+                nc.sync.dma_start(out=out[clip, rows, cols], in_=result[:])
 
         load_weight("p", p_w, p_b)
         load_x(0, 0)
         load_weight("t", t_w, t_b)
-        load_x(0, 1)
-        for piece in range(LOADS_PER_CLIP):
-            load_x(1, piece)
+        for chunk in range(1, CHUNKS):
+            load_x(0, chunk)
+        for chunk in range(CHUNKS):
+            load_x(1, chunk)
+
+        units = [("p", 0, 0), ("t", 0, 0), ("p", 0, 1), ("t", 0, 1), ("p", 0, 2), ("p", 0, 3), ("t", 0, 2), ("t", 0, 3)]
+        units += [(which, 1, chunk) for which in ("p", "t") for chunk in range(CHUNKS)]
 
         group_weight("p")
-        quantise_weight("p")
-        for chunk in range(LOAD_CHUNKS):
-            group_x(0, chunk, nc.vector.tensor_copy)
+        quantise_weight("p", 0)
+        quantise_weight("p", 1)
+        group_x(0, 0, nc.vector.tensor_copy)
+        quantise_weight("p", 2)
+        quantise_weight("p", 3)
+        quantise_x(0, 0)
         group_weight("t")
-        for chunk in range(LOAD_CHUNKS, CHUNKS):
+        for chunk in range(2, CHUNKS):
             group_x(0, chunk, nc.scalar.copy)
         for chunk in range(CHUNKS):
             group_x(1, chunk, nc.scalar.copy)
-
-        units = [
-            (which, 0, piece * LOAD_CHUNKS + k)
-            for piece in range(LOADS_PER_CLIP)
-            for which in ("p", "t")
-            for k in range(LOAD_CHUNKS)
-        ] + [(which, 1, chunk) for which in ("p", "t") for chunk in range(CHUNKS)]
+        project(*units[0])
+        quantise_weight("t", 0)
+        quantise_weight("t", 1)
+        group_x(0, 1, nc.vector.tensor_copy)
+        quantise_weight("t", 2)
+        quantise_weight("t", 3)
+        project(*units[1])
+        quantise_x(0, 1)
+        project(*units[2])
+        x_quantised = set([(0, 0), (0, 1)])
 
         def start(which, clip, chunk):
-            if (which, clip, chunk) == ("t", 0, 0):
-                quantise_weight("t")
-            if which == "p":
+            if (clip, chunk) not in x_quantised:
                 quantise_x(clip, chunk)
+                x_quantised.add((clip, chunk))
             project(which, clip, chunk)
 
         quantised = set()
         multiplied = set()
-        for unit in units[:AHEAD]:
-            start(*unit)
         for i in range(len(units) + 1):
             if i < len(units):
                 add_bias(*units[i])
@@ -231,7 +237,7 @@ def tile_stnonlocalgnlstage_pa_kernel(tc, x, t_w, t_b, p_w, p_b, out):
                 if all([("p", clip, c) in quantised for c in range(CHUNKS)]):
                     for c in range(CHUNKS):
                         if ("t", clip, c) in quantised and (clip, c) not in multiplied:
-                            affinity_rows(clip, c)
+                            affinity_rows(clip, c, 2 if (clip == CLIPS - 1 and c >= CHUNKS - 2) else 1)
                             multiplied.add((clip, c))
             if i + AHEAD < len(units):
                 start(*units[i + AHEAD])

@@ -87,6 +87,41 @@ def tile_stnonlocalgnlstage_pa_kernel(tc, x, t_w, t_b, p_w, p_b, out):
                     in_=flipped[:].rearrange("q g u n -> q g n u"),
                 )
 
+        def group_weight_by_passes(which):
+            words = w_raw[which][:].bitcast(F32).rearrange(
+                "n (m g q u) -> n m g u q", m=FEATURE_TILES, g=C_PASSES, u=2
+            )
+            for m in range(FEATURE_TILES):
+                w_grouped[which, m] = keep.tile(
+                    [P, C_PASSES * P * PACK], BF16, align_bytes=64, name="w_grouped_%s%d" % (which, m)
+                )
+                for g in range(C_PASSES):
+                    flipped = psum_wide.tile([P, 2, P], F32, name="flipped_pass", tag="wide")
+                    for u in range(2):
+                        nc.tensor.transpose(
+                            out=flipped[:, u, :], in_=words[:, m, g, u, :], identity=identity[:]
+                        )
+                    nc.scalar.copy(
+                        out=w_grouped[which, m][:, g * P * PACK : (g + 1) * P * PACK]
+                        .bitcast(F32)
+                        .rearrange("q (n u) -> q n u", u=2),
+                        in_=flipped[:].rearrange("q u n -> q n u"),
+                    )
+
+        def quantise_weight_pass(which, m, g):
+            if (m, g) == (0, 0):
+                w_codes[which] = keep.tile(
+                    [P, FEATURE_TILES, C_PASSES, P], U32, align_bytes=64, name="w_codes_%s" % which
+                )
+                w_scales[which] = keep.tile(
+                    [P, FEATURE_TILES, C_PASSES, P], U8, align_bytes=64, name="w_scales_%s" % which
+                )
+            nc.vector.quantize_mx(
+                out=w_codes[which][:, m, g, :].bitcast(FP8X4),
+                scales=w_scales[which][:, m, g, :],
+                in_=w_grouped[which, m][:, g * P * PACK : (g + 1) * P * PACK],
+            )
+
         def quantise_weight(which, m):
             if m == 0:
                 w_codes[which] = keep.tile(
@@ -203,17 +238,17 @@ def tile_stnonlocalgnlstage_pa_kernel(tc, x, t_w, t_b, p_w, p_b, out):
         quantise_weight("p", 2)
         quantise_weight("p", 3)
         quantise_x(0, 0)
-        group_weight("t")
+        group_weight_by_passes("t")
         for chunk in range(2, CHUNKS):
             group_x(0, chunk, nc.scalar.copy)
         for chunk in range(CHUNKS):
             group_x(1, chunk, nc.scalar.copy)
         project(*units[0])
-        quantise_weight("t", 0)
-        quantise_weight("t", 1)
-        group_x(0, 1, nc.vector.tensor_copy)
-        quantise_weight("t", 2)
-        quantise_weight("t", 3)
+        for m in range(FEATURE_TILES):
+            if m == FEATURE_TILES // 2:
+                group_x(0, 1, nc.vector.tensor_copy)
+            for g in range(C_PASSES):
+                quantise_weight_pass("t", m, g)
         project(*units[1])
         quantise_x(0, 1)
         project(*units[2])
@@ -237,7 +272,7 @@ def tile_stnonlocalgnlstage_pa_kernel(tc, x, t_w, t_b, p_w, p_b, out):
                 if all([("p", clip, c) in quantised for c in range(CHUNKS)]):
                     for c in range(CHUNKS):
                         if ("t", clip, c) in quantised and (clip, c) not in multiplied:
-                            affinity_rows(clip, c, 2 if (clip == CLIPS - 1 and c >= CHUNKS - 2) else 1)
+                            affinity_rows(clip, c, 2 if clip == CLIPS - 1 else 1)
                             multiplied.add((clip, c))
             if i + AHEAD < len(units):
                 start(*units[i + AHEAD])

@@ -26,6 +26,8 @@ CHUNK = 128
 CHUNKS = L // CHUNK
 CHUNK_FRAMES = CHUNK // GRID
 TP_BANKS = 4
+WARM_UP = 5
+BETWEEN_WEIGHTS = 2
 RUN = 4
 AHEAD = 3
 
@@ -42,6 +44,14 @@ def tile_stnonlocalgnlstage_pa_kernel(tc, x, t_w, t_b, p_w, p_b, out):
 
         identity = keep.tile([P, P], F32, name="identity")
         make_identity(nc, identity[:])
+
+        zeros = keep.tile([P, L], BF16, name="zeros")
+        nc.vector.memset(zeros[:], 0.0)
+        idle_sums = psum_tp.tile([P, L], F32, name="acc")
+
+        def keep_clock_up(passes):
+            for i in range(passes):
+                nc.tensor.matmul(out=idle_sums[:], lhsT=zeros[:, :P], rhs=zeros[:], start=True, stop=True)
 
         w_raw, bias, w_grouped, w_codes, w_scales = {}, {}, {}, {}, {}
         x_raw, x_grouped, x_codes, x_scales = {}, {}, {}, {}
@@ -231,7 +241,9 @@ def tile_stnonlocalgnlstage_pa_kernel(tc, x, t_w, t_b, p_w, p_b, out):
         units = [("p", 0, 0), ("t", 0, 0), ("p", 0, 1), ("t", 0, 1), ("p", 0, 2), ("p", 0, 3), ("t", 0, 2), ("t", 0, 3)]
         units += [(which, 1, chunk) for which in ("p", "t") for chunk in range(CHUNKS)]
 
+        keep_clock_up(WARM_UP)
         group_weight("p")
+        keep_clock_up(BETWEEN_WEIGHTS)
         quantise_weight("p", 0)
         quantise_weight("p", 1)
         group_x(0, 0, nc.vector.tensor_copy)

@@ -9,6 +9,7 @@ U32 = mybir.dt.uint32
 U8 = mybir.dt.uint8
 FP8X4 = mybir.dt.float8_e4m3fn_x4
 ADD = mybir.AluOpType.add
+IDENTITY = mybir.ActivationFunctionType.Identity
 
 P = 128
 PACK = 4
@@ -28,6 +29,7 @@ CHUNK_FRAMES = CHUNK // GRID
 TP_BANKS = 4
 WARM_UP = 5
 BETWEEN_WEIGHTS = 2
+SCALAR_LEAD = 2
 RUN = 4
 AHEAD = 3
 
@@ -188,13 +190,16 @@ def tile_stnonlocalgnlstage_pa_kernel(tc, x, t_w, t_b, p_w, p_b, out):
                         stop=(g == C_PASSES - 1),
                     )
 
-        def add_bias(which, clip, chunk):
-            if chunk == 0:
+        def make_tp_tiles(which, clip):
+            if (which, clip) not in tp_grouped:
                 tp_grouped[which, clip] = keep.tile(
                     [P, L, PACK], BF16, align_bytes=64, name="grouped_%s%d" % (which, clip)
                 )
                 tp_codes[which, clip] = keep.tile([P, L], U32, align_bytes=64, name="codes_%s%d" % (which, clip))
                 tp_scales[which, clip] = keep.tile([P, L], U8, align_bytes=64, name="scales_%s%d" % (which, clip))
+
+        def add_bias(which, clip, chunk):
+            make_tp_tiles(which, clip)
             positions = slice(chunk * CHUNK, (chunk + 1) * CHUNK)
             nc.vector.tensor_tensor(
                 out=tp_grouped[which, clip][:, positions, :],
@@ -202,6 +207,18 @@ def tile_stnonlocalgnlstage_pa_kernel(tc, x, t_w, t_b, p_w, p_b, out):
                 in1=bias[which][:].unsqueeze(1).to_broadcast([P, CHUNK, FEATURE_TILES]),
                 op=ADD,
             )
+
+        def add_bias_on_scalar(which, clip, chunk):
+            make_tp_tiles(which, clip)
+            positions = slice(chunk * CHUNK, (chunk + 1) * CHUNK)
+            for m in range(FEATURE_TILES):
+                nc.scalar.activation(
+                    out=tp_grouped[which, clip][:, positions, m],
+                    in_=acc[which, clip, chunk][:, m, :],
+                    func=IDENTITY,
+                    bias=bias[which][:, m : m + 1],
+                    scale=1.0,
+                )
 
         def quantise_tp(which, clip, chunk):
             positions = slice(chunk * CHUNK, (chunk + 1) * CHUNK)
@@ -274,17 +291,20 @@ def tile_stnonlocalgnlstage_pa_kernel(tc, x, t_w, t_b, p_w, p_b, out):
 
         quantised = set()
         multiplied = set()
+        scalar_units = (("p", 1, 0),)
         for i in range(len(units) + 1):
-            if i < len(units):
-                add_bias(*units[i])
-            if i > 0:
-                which, clip, chunk = units[i - 1]
-                quantise_tp(which, clip, chunk)
-                quantised.add(units[i - 1])
-                if all([("p", clip, c) in quantised for c in range(CHUNKS)]):
-                    for c in range(CHUNKS):
-                        if ("t", clip, c) in quantised and (clip, c) not in multiplied:
-                            affinity_rows(clip, c, 2 if clip == CLIPS - 1 else 1)
-                            multiplied.add((clip, c))
+            if i + SCALAR_LEAD < len(units) and units[i + SCALAR_LEAD] in scalar_units:
+                add_bias_on_scalar(*units[i + SCALAR_LEAD])
+            if i == len(units) or units[i] not in scalar_units:
+                if i < len(units):
+                    add_bias(*units[i])
+                for which, clip, chunk in [unit for unit in units[:i] if unit not in quantised]:
+                    quantise_tp(which, clip, chunk)
+                    quantised.add((which, clip, chunk))
+                    if all([("p", clip, c) in quantised for c in range(CHUNKS)]):
+                        for c in range(CHUNKS):
+                            if ("t", clip, c) in quantised and (clip, c) not in multiplied:
+                                affinity_rows(clip, c, 2 if clip == CLIPS - 1 else 1)
+                                multiplied.add((clip, c))
             if i + AHEAD < len(units):
                 start(*units[i + AHEAD])

@@ -47,26 +47,28 @@ def tile_stnonlocalgnlstage_pa_kernel(tc, x, t_w, t_b, p_w, p_b, out):
         identity = keep.tile([P, P], F32, name="identity")
         make_identity(nc, identity[:])
 
-        zeros = keep.tile([P, L], BF16, name="zeros")
+        zeros = keep.tile([P, P], BF16, name="zeros")
         nc.vector.memset(zeros[:], 0.0)
         idle_sums = psum_tp.tile([P, L], F32, name="acc")
 
         def keep_clock_up(passes):
             for i in range(passes):
-                nc.tensor.matmul(out=idle_sums[:], lhsT=zeros[:, :P], rhs=zeros[:], start=True, stop=True)
+                nc.tensor.matmul(out=idle_sums[:], lhsT=zeros[:], rhs=zeros[:, 0:1].to_broadcast([P, L]), start=True, stop=True)
 
         w_raw, bias, w_grouped, w_codes, w_scales = {}, {}, {}, {}, {}
         x_raw, x_grouped, x_codes, x_scales = {}, {}, {}, {}
         acc, tp_grouped, tp_codes, tp_scales = {}, {}, {}, {}
 
-        def load_weight(which, w, b):
+        def load_bias(which, b):
+            bias[which] = keep.tile([P, FEATURE_TILES], BF16, name="bias_%s" % which)
+            nc.sync.dma_start(out=bias[which][:], in_=b.rearrange("(n m) -> n m", m=FEATURE_TILES))
+
+        def load_weight(which, w):
             w_raw[which] = keep.tile([P, FEATURE_TILES * C], BF16, name="w_raw_%s" % which)
             w_rows = w.rearrange("(n m) c -> n (m c)", m=FEATURE_TILES)
             for m in range(FEATURE_TILES):
                 cols = slice(m * C, (m + 1) * C)
                 nc.sync.dma_start(out=w_raw[which][:, cols], in_=w_rows[:, cols])
-            bias[which] = keep.tile([P, FEATURE_TILES], BF16, name="bias_%s" % which)
-            nc.scalar.dma_start(out=bias[which][:], in_=b.rearrange("(n m) -> n m", m=FEATURE_TILES))
 
         def load_x(clip, chunk):
             x_raw[clip, chunk] = keep.tile(
@@ -247,9 +249,11 @@ def tile_stnonlocalgnlstage_pa_kernel(tc, x, t_w, t_b, p_w, p_b, out):
                 nc.scalar.copy(out=result[:], in_=affinity[:])
                 nc.sync.dma_start(out=out[clip, rows, cols], in_=result[:])
 
-        load_weight("p", p_w, p_b)
+        load_weight("p", p_w)
         load_x(0, 0)
-        load_weight("t", t_w, t_b)
+        load_weight("t", t_w)
+        load_bias("p", p_b)
+        load_bias("t", t_b)
         for chunk in range(1, CHUNKS):
             load_x(0, chunk)
         for chunk in range(CHUNKS):

@@ -26,10 +26,10 @@ FEATURE_TILES = FEATURES // P
 CHUNK = 128
 CHUNKS = L // CHUNK
 CHUNK_FRAMES = CHUNK // GRID
+PAIR = 2 * CHUNK
 TP_BANKS = 4
 WARM_UP = 5
 BETWEEN_WEIGHTS = 2
-SCALAR_LEAD = 2
 RUN = 4
 AHEAD = 3
 
@@ -57,7 +57,9 @@ def tile_stnonlocalgnlstage_pa_kernel(tc, x, t_w, t_b, p_w, p_b, out):
 
         w_raw, bias, w_grouped, w_codes, w_scales = {}, {}, {}, {}, {}
         x_raw, x_grouped, x_codes, x_scales = {}, {}, {}, {}
-        acc, tp_grouped, tp_codes, tp_scales = {}, {}, {}, {}
+        acc, pair_acc, flat, tp_grouped, tp_codes, tp_scales = {}, {}, {}, {}, {}, {}
+        pair_codes = keep.tile([P, C_PASSES, PAIR], U32, align_bytes=64, name="pair_codes")
+        pair_scales = keep.tile([P, C_PASSES, PAIR], U8, align_bytes=64, name="pair_scales")
 
         def load_bias(which, b):
             bias[which] = keep.tile([P, FEATURE_TILES], BF16, name="bias_%s" % which)
@@ -165,6 +167,15 @@ def tile_stnonlocalgnlstage_pa_kernel(tc, x, t_w, t_b, p_w, p_b, out):
                         ),
                     )
 
+        def quantise_pair_x(chunk):
+            cols = slice(chunk * CHUNK, (chunk + 1) * CHUNK)
+            for g in range(C_PASSES):
+                nc.vector.quantize_mx(
+                    out=pair_codes[:, g, cols].bitcast(FP8X4),
+                    scales=pair_scales[:, g, cols],
+                    in_=x_grouped[1, chunk][:, g].rearrange("q s j -> q (s j)"),
+                )
+
         def quantise_x(clip, chunk):
             x_codes[clip, chunk] = keep.tile(
                 [P, C_PASSES, CHUNK], U32, align_bytes=64, name="x_codes_%d_%d" % (clip, chunk)
@@ -200,37 +211,60 @@ def tile_stnonlocalgnlstage_pa_kernel(tc, x, t_w, t_b, p_w, p_b, out):
                 tp_codes[which, clip] = keep.tile([P, L], U32, align_bytes=64, name="codes_%s%d" % (which, clip))
                 tp_scales[which, clip] = keep.tile([P, L], U8, align_bytes=64, name="scales_%s%d" % (which, clip))
 
-        def add_bias(which, clip, chunk):
+        def add_bias(which, clip, chunk, first=0, count=CHUNK):
             make_tp_tiles(which, clip)
-            positions = slice(chunk * CHUNK, (chunk + 1) * CHUNK)
+            positions = slice(chunk * CHUNK + first, chunk * CHUNK + first + count)
             nc.vector.tensor_tensor(
                 out=tp_grouped[which, clip][:, positions, :],
-                in0=acc[which, clip, chunk][:].rearrange("n m r -> n r m"),
-                in1=bias[which][:].unsqueeze(1).to_broadcast([P, CHUNK, FEATURE_TILES]),
+                in0=acc[which, clip, chunk][:, :, first : first + count].rearrange("n m r -> n r m"),
+                in1=bias[which][:].unsqueeze(1).to_broadcast([P, count, FEATURE_TILES]),
                 op=ADD,
             )
 
-        def add_bias_on_scalar(which, clip, chunk):
-            make_tp_tiles(which, clip)
-            positions = slice(chunk * CHUNK, (chunk + 1) * CHUNK)
+        def project_pair(which):
+            for h in range(2):
+                pair_acc[which, h] = psum_wide.tile([P, 2, PAIR], F32, name="pair_acc", tag="wide")
+                for k in range(2):
+                    m = 2 * h + k
+                    for g in range(C_PASSES):
+                        nc.tensor.matmul_mx(
+                            out=pair_acc[which, h][:, k, :],
+                            lhsT=w_codes[which][:, m, g, :].bitcast(FP8X4),
+                            lhsT_scale=w_scales[which][:, m, g, :],
+                            rhs=pair_codes[:, g, :].bitcast(FP8X4),
+                            rhs_scale=pair_scales[:, g, :],
+                            start=(g == 0),
+                            stop=(g == C_PASSES - 1),
+                        )
+
+        def add_bias_to_pair(which):
+            make_tp_tiles(which, 1)
+            flat[which] = keep.tile([P, FEATURE_TILES, PAIR], BF16, name="flat_%s" % which)
             for m in range(FEATURE_TILES):
                 nc.scalar.activation(
-                    out=tp_grouped[which, clip][:, positions, m],
-                    in_=acc[which, clip, chunk][:, m, :],
+                    out=flat[which][:, m, :],
+                    in_=pair_acc[which, m // 2][:, m % 2, :],
                     func=IDENTITY,
                     bias=bias[which][:, m : m + 1],
                     scale=1.0,
                 )
 
-        def quantise_tp(which, clip, chunk):
+        def interleave(which, clip, chunk):
             positions = slice(chunk * CHUNK, (chunk + 1) * CHUNK)
+            nc.vector.tensor_copy(
+                out=tp_grouped[which, clip][:, positions, :].rearrange("n (c i) m -> n c m i", i=RUN),
+                in_=flat[which][:, :, positions].rearrange("n m (c i) -> n c m i", i=RUN),
+            )
+
+        def quantise_tp(which, clip, chunk, first=0, count=CHUNK):
+            positions = slice(chunk * CHUNK + first, chunk * CHUNK + first + count)
             nc.vector.quantize_mx(
                 out=tp_codes[which, clip][:, positions].bitcast(FP8X4),
                 scales=tp_scales[which, clip][:, positions],
                 in_=tp_grouped[which, clip][:, positions, :].rearrange("n r m -> n (r m)"),
             )
 
-        def affinity_rows(clip, chunk, pieces):
+        def affinity_rows(clip, chunk, pieces, copies=(nc.scalar.copy,)):
             rows = slice(chunk * CHUNK, (chunk + 1) * CHUNK)
             width = L // pieces
             for piece in range(pieces):
@@ -246,7 +280,7 @@ def tile_stnonlocalgnlstage_pa_kernel(tc, x, t_w, t_b, p_w, p_b, out):
                     stop=True,
                 )
                 result = keep.tile([P, width], F32, name="result_%d_%d_%d" % (clip, chunk, piece))
-                nc.scalar.copy(out=result[:], in_=affinity[:])
+                copies[piece % len(copies)](out=result[:], in_=affinity[:])
                 nc.sync.dma_start(out=out[clip, rows, cols], in_=result[:])
 
         load_weight("p", p_w)
@@ -295,20 +329,43 @@ def tile_stnonlocalgnlstage_pa_kernel(tc, x, t_w, t_b, p_w, p_b, out):
 
         quantised = set()
         multiplied = set()
-        scalar_units = (("p", 1, 0),)
-        for i in range(len(units) + 1):
-            if i + SCALAR_LEAD < len(units) and units[i + SCALAR_LEAD] in scalar_units:
-                add_bias_on_scalar(*units[i + SCALAR_LEAD])
-            if i == len(units) or units[i] not in scalar_units:
-                if i < len(units):
-                    add_bias(*units[i])
-                for which, clip, chunk in [unit for unit in units[:i] if unit not in quantised]:
-                    quantise_tp(which, clip, chunk)
-                    quantised.add((which, clip, chunk))
-                    if all([("p", clip, c) in quantised for c in range(CHUNKS)]):
-                        for c in range(CHUNKS):
-                            if ("t", clip, c) in quantised and (clip, c) not in multiplied:
-                                affinity_rows(clip, c, 2 if clip == CLIPS - 1 else 1)
-                                multiplied.add((clip, c))
-            if i + AHEAD < len(units):
+        pair_units = [(which, 1, chunk) for which in ("p", "t") for chunk in (0, 1)]
+        for i in range(len(units) - 1):
+            if units[i] in pair_units:
+                interleave(*units[i])
+            else:
+                add_bias(*units[i])
+            for which, clip, chunk in [unit for unit in units[:i] if unit not in quantised]:
+                quantise_tp(which, clip, chunk)
+                quantised.add((which, clip, chunk))
+            ready = [
+                (clip, c)
+                for clip in range(CLIPS)
+                for c in range(CHUNKS)
+                if ("t", clip, c) in quantised
+                and all([("p", clip, k) in quantised for k in range(CHUNKS)])
+                and (clip, c) not in multiplied
+            ]
+            if i == 6:
+                project_pair("t")
+                add_bias_to_pair("t")
+            for clip, c in ready[:1]:
+                affinity_rows(clip, c, 2 if clip == CLIPS - 1 else 1)
+                multiplied.add((clip, c))
+            if i + AHEAD < len(units) and units[i + AHEAD] not in pair_units:
                 start(*units[i + AHEAD])
+            if i == 3:
+                quantise_pair_x(0)
+            if i == 4:
+                quantise_pair_x(1)
+                project_pair("p")
+                add_bias_to_pair("p")
+
+        half = CHUNK // 2
+        add_bias(*units[-1], first=0, count=half)
+        quantise_tp(*units[-2])
+        affinity_rows(units[-2][1], units[-2][2], 2)
+        add_bias(*units[-1], first=half, count=half)
+        quantise_tp(*units[-1], first=0, count=half)
+        quantise_tp(*units[-1], first=half, count=half)
+        affinity_rows(units[-1][1], units[-1][2], 2, copies=(nc.scalar.copy, nc.vector.tensor_copy))

@@ -221,6 +221,8 @@ def tile_stnonlocalgnlstage_pa_kernel(tc, x, t_w, t_b, p_w, p_b, out):
                 op=ADD,
             )
 
+        pair_units = [(which, 1, chunk) for which in ("p", "t") for chunk in (0, 1)]
+
         def project_pair(which):
             for h in range(2):
                 pair_acc[which, h] = psum_wide.tile([P, 2, PAIR], F32, name="pair_acc", tag="wide")
@@ -249,11 +251,27 @@ def tile_stnonlocalgnlstage_pa_kernel(tc, x, t_w, t_b, p_w, p_b, out):
                     scale=1.0,
                 )
 
+        def add_bias_to_single(which, clip, chunk):
+            make_tp_tiles(which, clip)
+            flat[which, chunk] = keep.tile([P, FEATURE_TILES, CHUNK], BF16, name="flat_%s_%d" % (which, chunk))
+            for m in range(FEATURE_TILES):
+                nc.scalar.activation(
+                    out=flat[which, chunk][:, m, :],
+                    in_=acc[which, clip, chunk][:, m, :],
+                    func=IDENTITY,
+                    bias=bias[which][:, m : m + 1],
+                    scale=1.0,
+                )
+
         def interleave(which, clip, chunk):
             positions = slice(chunk * CHUNK, (chunk + 1) * CHUNK)
+            if (which, clip, chunk) in pair_units:
+                source = flat[which][:, :, positions]
+            else:
+                source = flat[which, chunk][:]
             nc.vector.tensor_copy(
                 out=tp_grouped[which, clip][:, positions, :].rearrange("n (c i) m -> n c m i", i=RUN),
-                in_=flat[which][:, :, positions].rearrange("n m (c i) -> n c m i", i=RUN),
+                in_=source.rearrange("n m (c i) -> n c m i", i=RUN),
             )
 
         def quantise_tp(which, clip, chunk, first=0, count=CHUNK):
@@ -329,9 +347,9 @@ def tile_stnonlocalgnlstage_pa_kernel(tc, x, t_w, t_b, p_w, p_b, out):
 
         quantised = set()
         multiplied = set()
-        pair_units = [(which, 1, chunk) for which in ("p", "t") for chunk in (0, 1)]
+        single = ("t", 1, 2)
         for i in range(len(units) - 1):
-            if units[i] in pair_units:
+            if units[i] in pair_units or units[i] == single:
                 interleave(*units[i])
             else:
                 add_bias(*units[i])
@@ -349,10 +367,16 @@ def tile_stnonlocalgnlstage_pa_kernel(tc, x, t_w, t_b, p_w, p_b, out):
             if i == 6:
                 project_pair("t")
                 add_bias_to_pair("t")
+            if i == 9:
+                if single[1:] not in x_quantised:
+                    quantise_x(*single[1:])
+                    x_quantised.add(single[1:])
+                project(*single)
+                add_bias_to_single(*single)
             for clip, c in ready[:1]:
                 affinity_rows(clip, c, 2 if clip == CLIPS - 1 else 1)
                 multiplied.add((clip, c))
-            if i + AHEAD < len(units) and units[i + AHEAD] not in pair_units:
+            if i + AHEAD < len(units) and units[i + AHEAD] not in pair_units + [single]:
                 start(*units[i + AHEAD])
             if i == 3:
                 quantise_pair_x(0)

@@ -28,7 +28,7 @@ CHUNKS = L // CHUNK
 CHUNK_FRAMES = CHUNK // GRID
 PAIR = 2 * CHUNK
 TP_BANKS = 4
-WARM_UP = 5
+WARM_UP = 4
 BETWEEN_WEIGHTS = 2
 RUN = 4
 AHEAD = 3

from contextlib import ExitStack

import concourse.mybir as mybir
from concourse.masks import make_identity

BF16 = mybir.dt.bfloat16
F32 = mybir.dt.float32
U32 = mybir.dt.uint32
U8 = mybir.dt.uint8
FP8X4 = mybir.dt.float8_e4m3fn_x4
ADD = mybir.AluOpType.add
IDENTITY = mybir.ActivationFunctionType.Identity

P = 128
PACK = 4
K_PASS = P * PACK

CLIPS = 2
GRID = 64
L = 512
C = 1024
C_PASSES = C // K_PASS
FEATURES = 512
FEATURE_TILES = FEATURES // P

CHUNK = 128
CHUNKS = L // CHUNK
CHUNK_FRAMES = CHUNK // GRID
PAIR = 2 * CHUNK
TP_BANKS = 4
WARM_UP = 4
BETWEEN_WEIGHTS = 2
RUN = 4
AHEAD = 3

FLOPS = 2 * 2 * CLIPS * L * C * FEATURES + 2 * CLIPS * L * L * FEATURES


def tile_stnonlocalgnlstage_pa_kernel(tc, x, t_w, t_b, p_w, p_b, out):
    nc = tc.nc
    with ExitStack() as stack:
        keep = stack.enter_context(tc.tile_pool(name="keep", bufs=1))
        psum_wide = stack.enter_context(tc.psum_pool(name="psum_wide", bufs=4))
        psum_tp = stack.enter_context(tc.psum_pool(name="psum_tp", bufs=TP_BANKS))
        stack.enter_context(tc.manual_schedule())

        identity = keep.tile([P, P], F32, name="identity")
        make_identity(nc, identity[:])

        zeros = keep.tile([P, P], BF16, name="zeros")
        nc.vector.memset(zeros[:], 0.0)
        idle_sums = psum_tp.tile([P, L], F32, name="acc")

        def keep_clock_up(passes):
            for i in range(passes):
                nc.tensor.matmul(out=idle_sums[:], lhsT=zeros[:], rhs=zeros[:, 0:1].to_broadcast([P, L]), start=True, stop=True)

        w_raw, bias, w_grouped, w_codes, w_scales = {}, {}, {}, {}, {}
        x_raw, x_grouped, x_codes, x_scales = {}, {}, {}, {}
        acc, pair_acc, flat, tp_grouped, tp_codes, tp_scales = {}, {}, {}, {}, {}, {}
        pair_codes = keep.tile([P, C_PASSES, PAIR], U32, align_bytes=64, name="pair_codes")
        pair_scales = keep.tile([P, C_PASSES, PAIR], U8, align_bytes=64, name="pair_scales")

        def load_bias(which, b):
            bias[which] = keep.tile([P, FEATURE_TILES], BF16, name="bias_%s" % which)
            nc.sync.dma_start(out=bias[which][:], in_=b.rearrange("(n m) -> n m", m=FEATURE_TILES))

        def load_weight(which, w):
            w_raw[which] = keep.tile([P, FEATURE_TILES * C], BF16, name="w_raw_%s" % which)
            w_rows = w.rearrange("(n m) c -> n (m c)", m=FEATURE_TILES)
            for m in range(FEATURE_TILES):
                cols = slice(m * C, (m + 1) * C)
                nc.sync.dma_start(out=w_raw[which][:, cols], in_=w_rows[:, cols])

        def load_x(clip, chunk):
            x_raw[clip, chunk] = keep.tile(
                [P, CHUNK_FRAMES, C_PASSES, PACK * GRID], BF16, name="x_raw_%d_%d" % (clip, chunk)
            )
            first = (clip * CHUNKS + chunk) * CHUNK_FRAMES
            nc.sync.dma_start(
                out=x_raw[clip, chunk][:].rearrange("q f g r -> q (f g) r"),
                in_=x[first : first + CHUNK_FRAMES].rearrange(
                    "f (g q j) h w -> q (f g) (j h w)", g=C_PASSES, j=PACK
                ),
            )

        def group_weight(which):
            words = w_raw[which][:].bitcast(F32).rearrange(
                "n (m g q u) -> n m g u q", m=FEATURE_TILES, g=C_PASSES, u=2
            )
            for m in range(FEATURE_TILES):
                flipped = psum_wide.tile([P, C_PASSES, 2, P], F32, name="flipped", tag="wide")
                for g in range(C_PASSES):
                    for u in range(2):
                        nc.tensor.transpose(
                            out=flipped[:, g, u, :], in_=words[:, m, g, u, :], identity=identity[:]
                        )
                w_grouped[which, m] = keep.tile(
                    [P, C_PASSES * P * PACK], BF16, align_bytes=64, name="w_grouped_%s%d" % (which, m)
                )
                nc.scalar.copy(
                    out=w_grouped[which, m][:].bitcast(F32).rearrange("q (g n u) -> q g n u", g=C_PASSES, u=2),
                    in_=flipped[:].rearrange("q g u n -> q g n u"),
                )

        def group_weight_by_passes(which):
            words = w_raw[which][:].bitcast(F32).rearrange(
                "n (m g q u) -> n m g u q", m=FEATURE_TILES, g=C_PASSES, u=2
            )
            for m in range(FEATURE_TILES):
                w_grouped[which, m] = keep.tile(
                    [P, C_PASSES * P * PACK], BF16, align_bytes=64, name="w_grouped_%s%d" % (which, m)
                )
                for g in range(C_PASSES):
                    flipped = psum_wide.tile([P, 2, P], F32, name="flipped_pass", tag="wide")
                    for u in range(2):
                        nc.tensor.transpose(
                            out=flipped[:, u, :], in_=words[:, m, g, u, :], identity=identity[:]
                        )
                    nc.scalar.copy(
                        out=w_grouped[which, m][:, g * P * PACK : (g + 1) * P * PACK]
                        .bitcast(F32)
                        .rearrange("q (n u) -> q n u", u=2),
                        in_=flipped[:].rearrange("q u n -> q n u"),
                    )

        def quantise_weight_pass(which, m, g):
            if (m, g) == (0, 0):
                w_codes[which] = keep.tile(
                    [P, FEATURE_TILES, C_PASSES, P], U32, align_bytes=64, name="w_codes_%s" % which
                )
                w_scales[which] = keep.tile(
                    [P, FEATURE_TILES, C_PASSES, P], U8, align_bytes=64, name="w_scales_%s" % which
                )
            nc.vector.quantize_mx(
                out=w_codes[which][:, m, g, :].bitcast(FP8X4),
                scales=w_scales[which][:, m, g, :],
                in_=w_grouped[which, m][:, g * P * PACK : (g + 1) * P * PACK],
            )

        def quantise_weight(which, m):
            if m == 0:
                w_codes[which] = keep.tile(
                    [P, FEATURE_TILES, C_PASSES, P], U32, align_bytes=64, name="w_codes_%s" % which
                )
                w_scales[which] = keep.tile(
                    [P, FEATURE_TILES, C_PASSES, P], U8, align_bytes=64, name="w_scales_%s" % which
                )
            nc.vector.quantize_mx(
                out=w_codes[which][:, m].rearrange("q g n -> q (g n)").bitcast(FP8X4),
                scales=w_scales[which][:, m].rearrange("q g n -> q (g n)"),
                in_=w_grouped[which, m][:],
            )

        def group_x(clip, chunk, copy):
            x_grouped[clip, chunk] = keep.tile(
                [P, C_PASSES, CHUNK, PACK], BF16, align_bytes=64, name="x_grouped_%d_%d" % (clip, chunk)
            )
            for g in range(C_PASSES):
                for f in range(CHUNK_FRAMES):
                    copy(
                        out=x_grouped[clip, chunk][:, g, f * GRID : (f + 1) * GRID, :].rearrange(
                            "q (c i) j -> q c j i", i=RUN
                        ),
                        in_=x_raw[clip, chunk][:, f, g].rearrange(
                            "q (j c i) -> q c j i", j=PACK, i=RUN
                        ),
                    )

        def quantise_pair_x(chunk):
            cols = slice(chunk * CHUNK, (chunk + 1) * CHUNK)
            for g in range(C_PASSES):
                nc.vector.quantize_mx(
                    out=pair_codes[:, g, cols].bitcast(FP8X4),
                    scales=pair_scales[:, g, cols],
                    in_=x_grouped[1, chunk][:, g].rearrange("q s j -> q (s j)"),
                )

        def quantise_x(clip, chunk):
            x_codes[clip, chunk] = keep.tile(
                [P, C_PASSES, CHUNK], U32, align_bytes=64, name="x_codes_%d_%d" % (clip, chunk)
            )
            x_scales[clip, chunk] = keep.tile(
                [P, C_PASSES, CHUNK], U8, align_bytes=64, name="x_scales_%d_%d" % (clip, chunk)
            )
            nc.vector.quantize_mx(
                out=x_codes[clip, chunk][:].rearrange("q g s -> q (g s)").bitcast(FP8X4),
                scales=x_scales[clip, chunk][:].rearrange("q g s -> q (g s)"),
                in_=x_grouped[clip, chunk][:].rearrange("q g s j -> q (g s j)"),
            )

        def project(which, clip, chunk):
            acc[which, clip, chunk] = psum_tp.tile([P, FEATURE_TILES, CHUNK], F32, name="acc")
            for m in range(FEATURE_TILES):
                for g in range(C_PASSES):
                    nc.tensor.matmul_mx(
                        out=acc[which, clip, chunk][:, m, :],
                        lhsT=w_codes[which][:, m, g, :].bitcast(FP8X4),
                        lhsT_scale=w_scales[which][:, m, g, :],
                        rhs=x_codes[clip, chunk][:, g, :].bitcast(FP8X4),
                        rhs_scale=x_scales[clip, chunk][:, g, :],
                        start=(g == 0),
                        stop=(g == C_PASSES - 1),
                    )

        def make_tp_tiles(which, clip):
            if (which, clip) not in tp_grouped:
                tp_grouped[which, clip] = keep.tile(
                    [P, L, PACK], BF16, align_bytes=64, name="grouped_%s%d" % (which, clip)
                )
                tp_codes[which, clip] = keep.tile([P, L], U32, align_bytes=64, name="codes_%s%d" % (which, clip))
                tp_scales[which, clip] = keep.tile([P, L], U8, align_bytes=64, name="scales_%s%d" % (which, clip))

        def add_bias(which, clip, chunk, first=0, count=CHUNK):
            make_tp_tiles(which, clip)
            positions = slice(chunk * CHUNK + first, chunk * CHUNK + first + count)
            nc.vector.tensor_tensor(
                out=tp_grouped[which, clip][:, positions, :],
                in0=acc[which, clip, chunk][:, :, first : first + count].rearrange("n m r -> n r m"),
                in1=bias[which][:].unsqueeze(1).to_broadcast([P, count, FEATURE_TILES]),
                op=ADD,
            )

        pair_units = [(which, 1, chunk) for which in ("p", "t") for chunk in (0, 1)]

        def project_pair(which):
            for h in range(2):
                pair_acc[which, h] = psum_wide.tile([P, 2, PAIR], F32, name="pair_acc", tag="wide")
                for k in range(2):
                    m = 2 * h + k
                    for g in range(C_PASSES):
                        nc.tensor.matmul_mx(
                            out=pair_acc[which, h][:, k, :],
                            lhsT=w_codes[which][:, m, g, :].bitcast(FP8X4),
                            lhsT_scale=w_scales[which][:, m, g, :],
                            rhs=pair_codes[:, g, :].bitcast(FP8X4),
                            rhs_scale=pair_scales[:, g, :],
                            start=(g == 0),
                            stop=(g == C_PASSES - 1),
                        )

        def add_bias_to_pair(which):
            make_tp_tiles(which, 1)
            flat[which] = keep.tile([P, FEATURE_TILES, PAIR], BF16, name="flat_%s" % which)
            for m in range(FEATURE_TILES):
                nc.scalar.activation(
                    out=flat[which][:, m, :],
                    in_=pair_acc[which, m // 2][:, m % 2, :],
                    func=IDENTITY,
                    bias=bias[which][:, m : m + 1],
                    scale=1.0,
                )

        def add_bias_to_single(which, clip, chunk):
            make_tp_tiles(which, clip)
            flat[which, chunk] = keep.tile([P, FEATURE_TILES, CHUNK], BF16, name="flat_%s_%d" % (which, chunk))
            for m in range(FEATURE_TILES):
                nc.scalar.activation(
                    out=flat[which, chunk][:, m, :],
                    in_=acc[which, clip, chunk][:, m, :],
                    func=IDENTITY,
                    bias=bias[which][:, m : m + 1],
                    scale=1.0,
                )

        def interleave(which, clip, chunk):
            positions = slice(chunk * CHUNK, (chunk + 1) * CHUNK)
            if (which, clip, chunk) in pair_units:
                source = flat[which][:, :, positions]
            else:
                source = flat[which, chunk][:]
            nc.vector.tensor_copy(
                out=tp_grouped[which, clip][:, positions, :].rearrange("n (c i) m -> n c m i", i=RUN),
                in_=source.rearrange("n m (c i) -> n c m i", i=RUN),
            )

        def quantise_tp(which, clip, chunk, first=0, count=CHUNK):
            positions = slice(chunk * CHUNK + first, chunk * CHUNK + first + count)
            nc.vector.quantize_mx(
                out=tp_codes[which, clip][:, positions].bitcast(FP8X4),
                scales=tp_scales[which, clip][:, positions],
                in_=tp_grouped[which, clip][:, positions, :].rearrange("n r m -> n (r m)"),
            )

        def affinity_rows(clip, chunk, pieces, copies=(nc.scalar.copy,)):
            rows = slice(chunk * CHUNK, (chunk + 1) * CHUNK)
            width = L // pieces
            for piece in range(pieces):
                cols = slice(piece * width, (piece + 1) * width)
                affinity = psum_wide.tile([P, width], F32, name="affinity", tag="wide")
                nc.tensor.matmul_mx(
                    out=affinity[:],
                    lhsT=tp_codes["t", clip][:, rows].bitcast(FP8X4),
                    lhsT_scale=tp_scales["t", clip][:, rows],
                    rhs=tp_codes["p", clip][:, cols].bitcast(FP8X4),
                    rhs_scale=tp_scales["p", clip][:, cols],
                    start=True,
                    stop=True,
                )
                result = keep.tile([P, width], F32, name="result_%d_%d_%d" % (clip, chunk, piece))
                copies[piece % len(copies)](out=result[:], in_=affinity[:])
                nc.sync.dma_start(out=out[clip, rows, cols], in_=result[:])

        load_weight("p", p_w)
        load_x(0, 0)
        load_weight("t", t_w)
        load_bias("p", p_b)
        load_bias("t", t_b)
        for chunk in range(1, CHUNKS):
            load_x(0, chunk)
        for chunk in range(CHUNKS):
            load_x(1, chunk)

        units = [("p", 0, 0), ("t", 0, 0), ("p", 0, 1), ("t", 0, 1), ("p", 0, 2), ("p", 0, 3), ("t", 0, 2), ("t", 0, 3)]
        units += [(which, 1, chunk) for which in ("p", "t") for chunk in range(CHUNKS)]

        keep_clock_up(WARM_UP)
        group_weight("p")
        keep_clock_up(BETWEEN_WEIGHTS)
        quantise_weight("p", 0)
        quantise_weight("p", 1)
        group_x(0, 0, nc.vector.tensor_copy)
        quantise_weight("p", 2)
        quantise_weight("p", 3)
        quantise_x(0, 0)
        group_weight_by_passes("t")
        for chunk in range(2, CHUNKS):
            group_x(0, chunk, nc.scalar.copy)
        for chunk in range(CHUNKS):
            group_x(1, chunk, nc.scalar.copy)
        project(*units[0])
        for m in range(FEATURE_TILES):
            if m == FEATURE_TILES // 2:
                group_x(0, 1, nc.vector.tensor_copy)
            for g in range(C_PASSES):
                quantise_weight_pass("t", m, g)
        project(*units[1])
        quantise_x(0, 1)
        project(*units[2])
        x_quantised = set([(0, 0), (0, 1)])

        def start(which, clip, chunk):
            if (clip, chunk) not in x_quantised:
                quantise_x(clip, chunk)
                x_quantised.add((clip, chunk))
            project(which, clip, chunk)

        quantised = set()
        multiplied = set()
        single = ("t", 1, 2)
        for i in range(len(units) - 1):
            if units[i] in pair_units or units[i] == single:
                interleave(*units[i])
            else:
                add_bias(*units[i])
            for which, clip, chunk in [unit for unit in units[:i] if unit not in quantised]:
                quantise_tp(which, clip, chunk)
                quantised.add((which, clip, chunk))
            ready = [
                (clip, c)
                for clip in range(CLIPS)
                for c in range(CHUNKS)
                if ("t", clip, c) in quantised
                and all([("p", clip, k) in quantised for k in range(CHUNKS)])
                and (clip, c) not in multiplied
            ]
            if i == 6:
                project_pair("t")
                add_bias_to_pair("t")
            if i == 9:
                if single[1:] not in x_quantised:
                    quantise_x(*single[1:])
                    x_quantised.add(single[1:])
                project(*single)
                add_bias_to_single(*single)
            for clip, c in ready[:1]:
                affinity_rows(clip, c, 2 if clip == CLIPS - 1 else 1)
                multiplied.add((clip, c))
            if i + AHEAD < len(units) and units[i + AHEAD] not in pair_units + [single]:
                start(*units[i + AHEAD])
            if i == 3:
                quantise_pair_x(0)
            if i == 4:
                quantise_pair_x(1)
                project_pair("p")
                add_bias_to_pair("p")

        half = CHUNK // 2
        add_bias(*units[-1], first=0, count=half)
        quantise_tp(*units[-2])
        affinity_rows(units[-2][1], units[-2][2], 2)
        add_bias(*units[-1], first=half, count=half)
        quantise_tp(*units[-1], first=0, count=half)
        quantise_tp(*units[-1], first=half, count=half)
        affinity_rows(units[-1][1], units[-1][2], 2, copies=(nc.scalar.copy, nc.vector.tensor_copy))
